import numpy as np
import ml_dtypes


def mxq(x, axis, fmt="e4m3"):
    dtype, down = {"e4m3": (ml_dtypes.float8_e4m3fn, 7), "e5m2": (ml_dtypes.float8_e5m2, 14)}[fmt]
    v = np.moveaxis(np.asarray(x, np.float32).astype(ml_dtypes.bfloat16).astype(np.float64), axis, -1)
    blocks = v.reshape(v.shape[:-1] + (-1, 32))
    amax = np.abs(blocks).max(-1, keepdims=True)
    byte = np.maximum(np.where(amax > 0, np.frexp(amax)[1] - 1 + 127, 0) - down, 1)
    scale = np.exp2(byte - 127.0)
    codes = (blocks / scale).astype(np.float32).astype(dtype).astype(np.float64)
    return np.moveaxis((codes * scale).reshape(v.shape), -1, axis)


WIDE = False


def mx_kscale(k):
    if not WIDE:
        return np.ones(k)
    levels = np.array([10, -10, 5, -5, 0])
    a = np.random.permutation(np.resize(levels, k // 512 * 4)).reshape(k // 512, 4)
    idx = np.arange(k)
    return np.exp2(a[idx // 512, idx % 128 // 32])


BF16 = ml_dtypes.bfloat16


def bf(x):
    return np.asarray(x, np.float32).astype(BF16)


def f64(x):
    return np.asarray(x).astype(np.float64)


B, F, M, N, H, O = 1, 128, 32, 128, 512, 128
BN_EPS = 1e-5


def bn(x, g, b, m, v):
    sh = [1] * x.ndim
    sh[1] = -1
    return g.reshape(sh) * (x - m.reshape(sh)) * (1.0 / np.sqrt(v.reshape(sh) + BN_EPS)) + b.reshape(sh)


def setup_inputs():
    s = mx_kscale(H)
    k = mx_kscale(H)
    return {"h2": bf(np.maximum(np.random.standard_normal((B, H, M, N)), 0.0) * s[None, :, None, None]),
            "W3": bf(np.random.standard_normal((H, H)) * 1.4 / np.sqrt(H) / s[None, :]),
            "g3": bf((1.0 + 0.1 * np.random.standard_normal(H)) * k),
            "b3": bf(0.2 * np.random.standard_normal(H) * k),
            "m3": bf(0.2 * np.random.standard_normal(H)),
            "v3": bf(np.random.uniform(0.5, 1.5, H)),
            "Wc1": bf(np.random.standard_normal((H, H)) * 0.4 / np.sqrt(H) / k[None, :]),
            "gc1": bf(1.0 + 0.1 * np.random.standard_normal(H)),
            "bc1": bf(0.2 * np.random.standard_normal(H)),
            "mc1": bf(0.2 * np.random.standard_normal(H)),
            "vc1": bf(np.random.uniform(0.5, 1.5, H))}


def reference(h2, W3, g3, b3, m3, v3, Wc1, gc1, bc1, mc1, vc1):
    x3 = (mxq(f64(W3), 1, "e4m3") @ mxq(f64(h2).reshape(B, H, M * N), 1, "e4m3")).reshape(B, H, M, N)
    h3 = np.maximum(bn(x3, f64(g3), f64(b3), f64(m3), f64(v3)), 0.0)
    p = h3.max(axis=2)
    xc = mxq(f64(Wc1), 1, "e4m3") @ mxq(p, 1, "e4m3")
    return np.maximum(bn(xc, f64(gc1), f64(bc1), f64(mc1), f64(vc1)), 0.0)

@@ -1,0 +1,199 @@
+from contextlib import ExitStack
+
+import concourse.mybir as mybir
+from concourse.masks import make_identity
+
+BF16 = mybir.dt.bfloat16
+F32 = mybir.dt.float32
+U32 = mybir.dt.uint32
+U8 = mybir.dt.uint8
+FP8X4 = mybir.dt.float8_e4m3fn_x4
+RELU = mybir.ActivationFunctionType.Relu
+
+P = 128
+PACK = 4
+H = P * PACK
+M_PTS = 32
+N_PTS = 128
+COLS = M_PTS * N_PTS
+BANK = 512
+CHUNKS = COLS // BANK
+WORDS = H // 2
+BN_EPS = 1e-5
+MERGE_LAG = 2
+
+FLOPS = 2 * H * H * (COLS + N_PTS)
+
+
+def tile_p2b_xcorr_pb_t_kernel(tc, h2, W3, g3, b3, m3, v3, Wc1, gc1, bc1, mc1, vc1, out):
+    nc = tc.nc
+    with ExitStack() as ctx:
+        keep = ctx.enter_context(tc.tile_pool(name="keep", bufs=1))
+        stage = ctx.enter_context(tc.tile_pool(name="stage", bufs=MERGE_LAG + 2))
+        psum_w = ctx.enter_context(tc.psum_pool(name="psum_w", bufs=2))
+        psum_x = ctx.enter_context(tc.psum_pool(name="psum_x", bufs=5))
+        psum_y = ctx.enter_context(tc.psum_pool(name="psum_y", bufs=1))
+        ctx.enter_context(tc.manual_schedule())
+
+        SLOT = 16
+        bn_raw = keep.tile([P, 8, SLOT], BF16, name="bn_raw")
+
+        def load_vector(slot, vec):
+            nc.scalar.dma_start(out=bn_raw[:, slot, 0:PACK], in_=vec.rearrange("(p j) -> p j", j=PACK))
+
+        for slot, vec in enumerate((v3, vc1, g3, gc1, m3)):
+            load_vector(slot, vec)
+        load_vector(6, b3)
+
+        h2_rows = h2[0].rearrange("(p j) m n -> p j (m n)", j=PACK)
+        w3_rows = keep.tile([P, PACK * H], BF16, name="w3_rows")
+        wc1_rows = keep.tile([P, PACK * H], BF16, name="wc1_rows")
+        h2_raw = [keep.tile([P, PACK, BANK], BF16, name="h2_raw%d" % c) for c in range(CHUNKS)]
+
+        def load_chunk(c):
+            nc.sync.dma_start(out=h2_raw[c][:], in_=h2_rows[:, :, c * BANK : (c + 1) * BANK])
+
+        nc.sync.dma_start(out=w3_rows[:], in_=W3.rearrange("(p j) h -> p (j h)", j=PACK))
+        load_chunk(0)
+
+        ident = keep.tile([P, P], F32, name="ident")
+        make_identity(nc, ident[:])
+        warm = keep.tile([P, 1], F32, name="warm")
+        nc.vector.memset(warm[:], 1.0)
+        nc.scalar.sqrt(out=warm[:], in_=warm[:])
+
+        load_vector(5, mc1)
+        load_vector(7, bc1)
+        load_chunk(1)
+        nc.sync.dma_start(out=wc1_rows[:], in_=Wc1.rearrange("(p j) h -> p (j h)", j=PACK))
+        for c in range(2, CHUNKS):
+            load_chunk(c)
+
+        scale = keep.tile([P, 2, PACK], F32, name="scale")
+        shift = keep.tile([P, 2, PACK], F32, name="shift")
+        nc.vector.tensor_scalar_add(out=scale[:], in0=bn_raw[:, 0:2, 0:PACK], scalar1=BN_EPS)
+        nc.scalar.sqrt(out=scale[:], in_=scale[:])
+        nc.vector.reciprocal(out=scale[:], in_=scale[:])
+        nc.vector.tensor_mul(out=scale[:], in0=scale[:], in1=bn_raw[:, 2:4, 0:PACK])
+
+        def fold_shift(i):
+            nc.vector.tensor_mul(out=shift[:, i, :], in0=scale[:, i, :], in1=bn_raw[:, 4 + i, 0:PACK])
+            nc.vector.tensor_sub(out=shift[:, i, :], in0=bn_raw[:, 6 + i, 0:PACK], in1=shift[:, i, :])
+
+        fold_shift(0)
+
+        def flip_weight(rows, name):
+            words = rows[:].bitcast(F32)
+            grouped = keep.tile([P, PACK * P * PACK], BF16, name=name, align_bytes=64)
+            grouped_words = grouped[:].bitcast(F32).rearrange("q (j p u) -> q j p u", j=PACK, u=2)
+            for j_pair in range(0, PACK, 2):
+                flipped = psum_w.tile([P, 2, 2, P], F32, name="flipped")
+                for j in range(2):
+                    first = (j_pair + j) * WORDS
+                    for u in range(2):
+                        nc.tensor.transpose(flipped[:, j, u, :], words[:, first + u : first + WORDS : 2], ident[:])
+                nc.scalar.copy(
+                    out=grouped_words[:, j_pair : j_pair + 2, :, :],
+                    in_=flipped[:].rearrange("q j u p -> q j p u"),
+                )
+            return grouped
+
+        def quantise_weight(grouped, name):
+            codes = keep.tile([P, H], U32, name=name + "_codes", align_bytes=64)
+            scales = keep.tile([P, H], U8, name=name + "_scales", align_bytes=64)
+            nc.vector.quantize_mx(out=codes[:].bitcast(FP8X4), scales=scales[:], in_=grouped[:])
+            return codes, scales
+
+        h2_codes = keep.tile([P, CHUNKS, BANK], U32, name="h2_codes", align_bytes=64)
+        h2_scales = keep.tile([P, CHUNKS, BANK], U8, name="h2_scales", align_bytes=64)
+        h2_grouped = {}
+
+        def regroup(c):
+            grouped = stage.tile([P, BANK, PACK], BF16, name="h2_grouped", align_bytes=64)
+            nc.vector.tensor_copy(
+                out=grouped[:].rearrange("p (c i) j -> p c j i", i=4),
+                in_=h2_raw[c][:].rearrange("p j (c i) -> p c j i", i=4),
+            )
+            h2_grouped[c] = grouped
+
+        def quantise(c):
+            nc.vector.quantize_mx(
+                out=h2_codes[:, c, :].bitcast(FP8X4),
+                scales=h2_scales[:, c, :],
+                in_=h2_grouped[c][:].rearrange("p c j -> p (c j)"),
+            )
+
+        best = keep.tile([P, PACK, BANK], BF16, name="best")
+        h3_of = {0: best}
+
+        def conv3(c):
+            if c > 0:
+                h3_of[c] = stage.tile([P, PACK, BANK], BF16, name="h3")
+            for j in range(PACK):
+                x3 = psum_x.tile([P, BANK], F32, name="x3")
+                nc.tensor.matmul_mx(
+                    out=x3[:],
+                    lhsT=w3_codes[:, j * P : (j + 1) * P].bitcast(FP8X4),
+                    lhsT_scale=w3_scales[:, j * P : (j + 1) * P],
+                    rhs=h2_codes[:, c, :].bitcast(FP8X4),
+                    rhs_scale=h2_scales[:, c, :],
+                    start=True,
+                    stop=True,
+                )
+                nc.scalar.activation(
+                    out=h3_of[c][:, j, :], in_=x3[:], func=RELU,
+                    bias=shift[:, 0, j : j + 1], scale=scale[:, 0, j : j + 1],
+                )
+
+        def merge(c):
+            nc.vector.tensor_max(out=best[:], in0=best[:], in1=h3_of[c][:])
+
+        regroup(0)
+        w3_codes, w3_scales = quantise_weight(flip_weight(w3_rows, "w3_grouped"), "w3")
+        regroup(1)
+        wc1_grouped = flip_weight(wc1_rows, "wc1_grouped")
+        for c in range(CHUNKS):
+            quantise(c)
+            conv3(c)
+            if c - MERGE_LAG >= 1:
+                merge(c - MERGE_LAG)
+            if c + 2 < CHUNKS:
+                regroup(c + 2)
+        for c in range(CHUNKS - MERGE_LAG, CHUNKS - 1):
+            merge(c)
+        wc1_codes, wc1_scales = quantise_weight(wc1_grouped, "wc1")
+        merge(CHUNKS - 1)
+
+        two = keep.tile([P, PACK, 2 * N_PTS], BF16, name="two")
+        nc.vector.tensor_max(out=two[:], in0=best[:, :, 0 : 2 * N_PTS], in1=best[:, :, 2 * N_PTS : BANK])
+        p_grouped = keep.tile([P, N_PTS, PACK], BF16, name="p_grouped", align_bytes=64)
+        nc.vector.tensor_max(
+            out=p_grouped[:],
+            in0=two[:, :, 0:N_PTS].rearrange("p j n -> p n j"),
+            in1=two[:, :, N_PTS : 2 * N_PTS].rearrange("p j n -> p n j"),
+        )
+        fold_shift(1)
+        p_codes = keep.tile([P, N_PTS], U32, name="p_codes", align_bytes=64)
+        p_scales = keep.tile([P, N_PTS], U8, name="p_scales", align_bytes=64)
+        nc.vector.quantize_mx(
+            out=p_codes[:].bitcast(FP8X4), scales=p_scales[:], in_=p_grouped[:].rearrange("p n j -> p (n j)")
+        )
+
+        xc = psum_y.tile([P, PACK, N_PTS], F32, name="xc")
+        result = keep.tile([P, PACK, N_PTS], F32, name="result")
+        for j in range(PACK):
+            nc.tensor.matmul_mx(
+                out=xc[:, j, :],
+                lhsT=wc1_codes[:, j * P : (j + 1) * P].bitcast(FP8X4),
+                lhsT_scale=wc1_scales[:, j * P : (j + 1) * P],
+                rhs=p_codes[:].bitcast(FP8X4),
+                rhs_scale=p_scales[:],
+                start=True,
+                stop=True,
+            )
+        for j in range(PACK):
+            nc.scalar.activation(
+                out=result[:, j, :], in_=xc[:, j, :], func=RELU,
+                bias=shift[:, 1, j : j + 1], scale=scale[:, 1, j : j + 1],
+            )
+        nc.sync.dma_start(out=out[0].rearrange("(p j) n -> p j n", j=PACK), in_=result[:])

@@ -33,7 +33,6 @@ def tile_p2b_xcorr_pb_t_kernel(tc, h2, W3, g3, b3, m3, v3, Wc1, gc1, bc1, mc1, v
         psum_w = ctx.enter_context(tc.psum_pool(name="psum_w", bufs=2))
         psum_x = ctx.enter_context(tc.psum_pool(name="psum_x", bufs=5))
         psum_y = ctx.enter_context(tc.psum_pool(name="psum_y", bufs=1))
-        ctx.enter_context(tc.manual_schedule())
 
         SLOT = 16
         bn_raw = keep.tile([P, 8, SLOT], BF16, name="bn_raw")

@@ -31,8 +31,9 @@ def tile_p2b_xcorr_pb_t_kernel(tc, h2, W3, g3, b3, m3, v3, Wc1, gc1, bc1, mc1, v
         keep = ctx.enter_context(tc.tile_pool(name="keep", bufs=1))
         stage = ctx.enter_context(tc.tile_pool(name="stage", bufs=MERGE_LAG + 2))
         psum_w = ctx.enter_context(tc.psum_pool(name="psum_w", bufs=2))
-        psum_x = ctx.enter_context(tc.psum_pool(name="psum_x", bufs=5))
-        psum_y = ctx.enter_context(tc.psum_pool(name="psum_y", bufs=1))
+        psum_x = ctx.enter_context(tc.psum_pool(name="psum_x", bufs=4))
+        psum_y = ctx.enter_context(tc.psum_pool(name="psum_y", bufs=2))
+        ctx.enter_context(tc.manual_schedule())
 
         SLOT = 16
         bn_raw = keep.tile([P, 8, SLOT], BF16, name="bn_raw")
@@ -178,21 +179,32 @@ def tile_p2b_xcorr_pb_t_kernel(tc, h2, W3, g3, b3, m3, v3, Wc1, gc1, bc1, mc1, v
             out=p_codes[:].bitcast(FP8X4), scales=p_scales[:], in_=p_grouped[:].rearrange("p n j -> p (n j)")
         )
 
-        xc = psum_y.tile([P, PACK, N_PTS], F32, name="xc")
+        xc_of = [psum_y.tile([P, PACK // 2, N_PTS], F32, name="xc") for parity in range(2)]
         result = keep.tile([P, PACK, N_PTS], F32, name="result")
-        for j in range(PACK):
-            nc.tensor.matmul_mx(
-                out=xc[:, j, :],
-                lhsT=wc1_codes[:, j * P : (j + 1) * P].bitcast(FP8X4),
-                lhsT_scale=wc1_scales[:, j * P : (j + 1) * P],
-                rhs=p_codes[:].bitcast(FP8X4),
-                rhs_scale=p_scales[:],
-                start=True,
-                stop=True,
-            )
-        for j in range(PACK):
+        out_rows = out[0].rearrange("(p j) n -> p j n", j=PACK)
+        for parity in range(2):
+            for j in range(parity, PACK, 2):
+                nc.tensor.matmul_mx(
+                    out=xc_of[parity][:, j // 2, :],
+                    lhsT=wc1_codes[:, j * P : (j + 1) * P].bitcast(FP8X4),
+                    lhsT_scale=wc1_scales[:, j * P : (j + 1) * P],
+                    rhs=p_codes[:].bitcast(FP8X4),
+                    rhs_scale=p_scales[:],
+                    start=True,
+                    stop=True,
+                )
+        for j in range(0, PACK, 2):
             nc.scalar.activation(
-                out=result[:, j, :], in_=xc[:, j, :], func=RELU,
+                out=result[:, j, :], in_=xc_of[0][:, j // 2, :], func=RELU,
                 bias=shift[:, 1, j : j + 1], scale=scale[:, 1, j : j + 1],
             )
-        nc.sync.dma_start(out=out[0].rearrange("(p j) n -> p j n", j=PACK), in_=result[:])
+            nc.sync.dma_start(out=out_rows[:, j, :], in_=result[:, j, :])
+        for j in range(1, PACK, 2):
+            nc.vector.tensor_scalar(
+                out=result[:, j, :], in0=xc_of[1][:, j // 2, :],
+                scalar1=scale[:, 1, j : j + 1], scalar2=shift[:, 1, j : j + 1],
+                op0=mybir.AluOpType.mult, op1=mybir.AluOpType.add,
+            )
+        nc.vector.tensor_scalar_max(out=result[:, 1:PACK:2, :], in0=result[:, 1:PACK:2, :], scalar1=0.0)
+        for j in range(1, PACK, 2):
+            nc.sync.dma_start(out=out_rows[:, j, :], in_=result[:, j, :])

@@ -41,9 +41,8 @@ def tile_p2b_xcorr_pb_t_kernel(tc, h2, W3, g3, b3, m3, v3, Wc1, gc1, bc1, mc1, v
         def load_vector(slot, vec):
             nc.scalar.dma_start(out=bn_raw[:, slot, 0:PACK], in_=vec.rearrange("(p j) -> p j", j=PACK))
 
-        for slot, vec in enumerate((v3, vc1, g3, gc1, m3)):
-            load_vector(slot, vec)
-        load_vector(6, b3)
+        def load_late_vector(slot, vec):
+            nc.sync.dma_start(out=bn_raw[:, slot, 0:PACK], in_=vec.rearrange("(p j) -> p j", j=PACK))
 
         h2_rows = h2[0].rearrange("(p j) m n -> p j (m n)", j=PACK)
         w3_rows = keep.tile([P, PACK * H], BF16, name="w3_rows")
@@ -53,34 +52,43 @@ def tile_p2b_xcorr_pb_t_kernel(tc, h2, W3, g3, b3, m3, v3, Wc1, gc1, bc1, mc1, v
         def load_chunk(c):
             nc.sync.dma_start(out=h2_raw[c][:], in_=h2_rows[:, :, c * BANK : (c + 1) * BANK])
 
-        nc.sync.dma_start(out=w3_rows[:], in_=W3.rearrange("(p j) h -> p (j h)", j=PACK))
         load_chunk(0)
+        nc.sync.dma_start(out=w3_rows[:], in_=W3.rearrange("(p j) h -> p (j h)", j=PACK))
+        load_chunk(1)
+        for slot, vec in ((0, v3), (1, vc1)):
+            load_vector(slot, vec)
 
+        warm = keep.tile([P, 1], F32, name="warm")
+        nc.gpsimd.memset(warm[:], 1.0)
+        nc.scalar.sqrt(out=warm[:], in_=warm[:])
+        for slot, vec in ((2, g3), (3, gc1), (4, m3), (6, b3)):
+            load_vector(slot, vec)
         ident = keep.tile([P, P], F32, name="ident")
         make_identity(nc, ident[:])
-        warm = keep.tile([P, 1], F32, name="warm")
-        nc.vector.memset(warm[:], 1.0)
-        nc.scalar.sqrt(out=warm[:], in_=warm[:])
 
-        load_vector(5, mc1)
-        load_vector(7, bc1)
-        load_chunk(1)
-        nc.sync.dma_start(out=wc1_rows[:], in_=Wc1.rearrange("(p j) h -> p (j h)", j=PACK))
         for c in range(2, CHUNKS):
             load_chunk(c)
+        nc.sync.dma_start(out=wc1_rows[:], in_=Wc1.rearrange("(p j) h -> p (j h)", j=PACK))
+        for slot, vec in ((5, mc1), (7, bc1)):
+            load_late_vector(slot, vec)
 
+        spread = keep.tile([P, 2, PACK], F32, name="spread")
+        root = keep.tile([P, 2, PACK], F32, name="root")
+        inverse = keep.tile([P, 2, PACK], F32, name="inverse")
         scale = keep.tile([P, 2, PACK], F32, name="scale")
+        moved = keep.tile([P, 2, PACK], F32, name="moved")
         shift = keep.tile([P, 2, PACK], F32, name="shift")
-        nc.vector.tensor_scalar_add(out=scale[:], in0=bn_raw[:, 0:2, 0:PACK], scalar1=BN_EPS)
-        nc.scalar.sqrt(out=scale[:], in_=scale[:])
-        nc.vector.reciprocal(out=scale[:], in_=scale[:])
-        nc.vector.tensor_mul(out=scale[:], in0=scale[:], in1=bn_raw[:, 2:4, 0:PACK])
+        nc.gpsimd.tensor_scalar_add(out=spread[:], in0=bn_raw[:, 0:2, 0:PACK], scalar1=BN_EPS)
+        nc.scalar.sqrt(out=root[:], in_=spread[:])
+
+        def fold_scale():
+            nc.vector.reciprocal(out=inverse[:], in_=root[:])
+            nc.gpsimd.tensor_mul(out=scale[:], in0=inverse[:], in1=bn_raw[:, 2:4, 0:PACK])
 
         def fold_shift(i):
-            nc.vector.tensor_mul(out=shift[:, i, :], in0=scale[:, i, :], in1=bn_raw[:, 4 + i, 0:PACK])
-            nc.vector.tensor_sub(out=shift[:, i, :], in0=bn_raw[:, 6 + i, 0:PACK], in1=shift[:, i, :])
+            nc.gpsimd.tensor_mul(out=moved[:, i, :], in0=scale[:, i, :], in1=bn_raw[:, 4 + i, 0:PACK])
+            nc.gpsimd.tensor_sub(out=shift[:, i, :], in0=bn_raw[:, 6 + i, 0:PACK], in1=moved[:, i, :])
 
-        fold_shift(0)
 
         def flip_weight(rows, name):
             words = rows[:].bitcast(F32)
@@ -98,11 +106,17 @@ def tile_p2b_xcorr_pb_t_kernel(tc, h2, W3, g3, b3, m3, v3, Wc1, gc1, bc1, mc1, v
                 )
             return grouped
 
-        def quantise_weight(grouped, name):
+        def weight_tiles(name):
             codes = keep.tile([P, H], U32, name=name + "_codes", align_bytes=64)
             scales = keep.tile([P, H], U8, name=name + "_scales", align_bytes=64)
-            nc.vector.quantize_mx(out=codes[:].bitcast(FP8X4), scales=scales[:], in_=grouped[:])
             return codes, scales
+
+        def quantise_weight(grouped, codes, scales, first, count):
+            cols = slice(first * P, (first + count) * P)
+            nc.vector.quantize_mx(
+                out=codes[:, cols].bitcast(FP8X4), scales=scales[:, cols],
+                in_=grouped[:, first * P * PACK : (first + count) * P * PACK],
+            )
 
         h2_codes = keep.tile([P, CHUNKS, BANK], U32, name="h2_codes", align_bytes=64)
         h2_scales = keep.tile([P, CHUNKS, BANK], U8, name="h2_scales", align_bytes=64)
@@ -148,20 +162,29 @@ def tile_p2b_xcorr_pb_t_kernel(tc, h2, W3, g3, b3, m3, v3, Wc1, gc1, bc1, mc1, v
         def merge(c):
             nc.vector.tensor_max(out=best[:], in0=best[:], in1=h3_of[c][:])
 
+        w3_codes, w3_scales = weight_tiles("w3")
+        wc1_codes, wc1_scales = weight_tiles("wc1")
         regroup(0)
-        w3_codes, w3_scales = quantise_weight(flip_weight(w3_rows, "w3_grouped"), "w3")
+        fold_scale()
+        fold_shift(0)
+        fold_shift(1)
+        w3_grouped = flip_weight(w3_rows, "w3_grouped")
+        quantise(0)
+        quantise_weight(w3_grouped, w3_codes, w3_scales, 0, 2)
         regroup(1)
-        wc1_grouped = flip_weight(wc1_rows, "wc1_grouped")
+        quantise_weight(w3_grouped, w3_codes, w3_scales, 2, 2)
+        regroup(2)
         for c in range(CHUNKS):
-            quantise(c)
             conv3(c)
-            if c - MERGE_LAG >= 1:
-                merge(c - MERGE_LAG)
-            if c + 2 < CHUNKS:
-                regroup(c + 2)
-        for c in range(CHUNKS - MERGE_LAG, CHUNKS - 1):
-            merge(c)
-        wc1_codes, wc1_scales = quantise_weight(wc1_grouped, "wc1")
+            if c == CHUNKS // 2 - 1:
+                wc1_grouped = flip_weight(wc1_rows, "wc1_grouped")
+            if c + 1 < CHUNKS:
+                quantise(c + 1)
+            if c + 1 - MERGE_LAG >= 1:
+                merge(c + 1 - MERGE_LAG)
+            if c + 3 < CHUNKS:
+                regroup(c + 3)
+        quantise_weight(wc1_grouped, wc1_codes, wc1_scales, 0, PACK)
         merge(CHUNKS - 1)
 
         two = keep.tile([P, PACK, 2 * N_PTS], BF16, name="two")
@@ -172,39 +195,28 @@ def tile_p2b_xcorr_pb_t_kernel(tc, h2, W3, g3, b3, m3, v3, Wc1, gc1, bc1, mc1, v
             in0=two[:, :, 0:N_PTS].rearrange("p j n -> p n j"),
             in1=two[:, :, N_PTS : 2 * N_PTS].rearrange("p j n -> p n j"),
         )
-        fold_shift(1)
         p_codes = keep.tile([P, N_PTS], U32, name="p_codes", align_bytes=64)
         p_scales = keep.tile([P, N_PTS], U8, name="p_scales", align_bytes=64)
         nc.vector.quantize_mx(
             out=p_codes[:].bitcast(FP8X4), scales=p_scales[:], in_=p_grouped[:].rearrange("p n j -> p (n j)")
         )
 
-        xc_of = [psum_y.tile([P, PACK // 2, N_PTS], F32, name="xc") for parity in range(2)]
+        xc_of = [psum_y.tile([P, PACK // 2, N_PTS], F32, name="xc") for half in range(2)]
         result = keep.tile([P, PACK, N_PTS], F32, name="result")
         out_rows = out[0].rearrange("(p j) n -> p j n", j=PACK)
-        for parity in range(2):
-            for j in range(parity, PACK, 2):
-                nc.tensor.matmul_mx(
-                    out=xc_of[parity][:, j // 2, :],
-                    lhsT=wc1_codes[:, j * P : (j + 1) * P].bitcast(FP8X4),
-                    lhsT_scale=wc1_scales[:, j * P : (j + 1) * P],
-                    rhs=p_codes[:].bitcast(FP8X4),
-                    rhs_scale=p_scales[:],
-                    start=True,
-                    stop=True,
-                )
-        for j in range(0, PACK, 2):
+        for j in range(PACK):
+            nc.tensor.matmul_mx(
+                out=xc_of[j // 2][:, j % 2, :],
+                lhsT=wc1_codes[:, j * P : (j + 1) * P].bitcast(FP8X4),
+                lhsT_scale=wc1_scales[:, j * P : (j + 1) * P],
+                rhs=p_codes[:].bitcast(FP8X4),
+                rhs_scale=p_scales[:],
+                start=True,
+                stop=True,
+            )
+        for j in range(PACK):
             nc.scalar.activation(
-                out=result[:, j, :], in_=xc_of[0][:, j // 2, :], func=RELU,
+                out=result[:, j, :], in_=xc_of[j // 2][:, j % 2, :], func=RELU,
                 bias=shift[:, 1, j : j + 1], scale=scale[:, 1, j : j + 1],
             )
-            nc.sync.dma_start(out=out_rows[:, j, :], in_=result[:, j, :])
-        for j in range(1, PACK, 2):
-            nc.vector.tensor_scalar(
-                out=result[:, j, :], in0=xc_of[1][:, j // 2, :],
-                scalar1=scale[:, 1, j : j + 1], scalar2=shift[:, 1, j : j + 1],
-                op0=mybir.AluOpType.mult, op1=mybir.AluOpType.add,
-            )
-        nc.vector.tensor_scalar_max(out=result[:, 1:PACK:2, :], in0=result[:, 1:PACK:2, :], scalar1=0.0)
-        for j in range(1, PACK, 2):
             nc.sync.dma_start(out=out_rows[:, j, :], in_=result[:, j, :])

@@ -76,18 +76,18 @@ def tile_p2b_xcorr_pb_t_kernel(tc, h2, W3, g3, b3, m3, v3, Wc1, gc1, bc1, mc1, v
         root = keep.tile([P, 2, PACK], F32, name="root")
         inverse = keep.tile([P, 2, PACK], F32, name="inverse")
         scale = keep.tile([P, 2, PACK], F32, name="scale")
-        moved = keep.tile([P, 2, PACK], F32, name="moved")
-        shift = keep.tile([P, 2, PACK], F32, name="shift")
-        nc.gpsimd.tensor_scalar_add(out=spread[:], in0=bn_raw[:, 0:2, 0:PACK], scalar1=BN_EPS)
+        moved = [keep.tile([P, PACK], F32, name="moved%d" % i) for i in range(2)]
+        shift = [keep.tile([P, PACK], F32, name="shift%d" % i) for i in range(2)]
+        nc.vector.tensor_scalar_add(out=spread[:], in0=bn_raw[:, 0:2, 0:PACK], scalar1=BN_EPS)
         nc.scalar.sqrt(out=root[:], in_=spread[:])
 
         def fold_scale():
             nc.vector.reciprocal(out=inverse[:], in_=root[:])
-            nc.gpsimd.tensor_mul(out=scale[:], in0=inverse[:], in1=bn_raw[:, 2:4, 0:PACK])
+            nc.vector.tensor_mul(out=scale[:], in0=inverse[:], in1=bn_raw[:, 2:4, 0:PACK])
 
-        def fold_shift(i):
-            nc.gpsimd.tensor_mul(out=moved[:, i, :], in0=scale[:, i, :], in1=bn_raw[:, 4 + i, 0:PACK])
-            nc.gpsimd.tensor_sub(out=shift[:, i, :], in0=bn_raw[:, 6 + i, 0:PACK], in1=moved[:, i, :])
+        def fold_shift(engine, i):
+            engine.tensor_mul(out=moved[i][:], in0=scale[:, i, :], in1=bn_raw[:, 4 + i, 0:PACK])
+            engine.tensor_sub(out=shift[i][:], in0=bn_raw[:, 6 + i, 0:PACK], in1=moved[i][:])
 
 
         def flip_weight(rows, name):
@@ -156,7 +156,7 @@ def tile_p2b_xcorr_pb_t_kernel(tc, h2, W3, g3, b3, m3, v3, Wc1, gc1, bc1, mc1, v
                 )
                 nc.scalar.activation(
                     out=h3_of[c][:, j, :], in_=x3[:], func=RELU,
-                    bias=shift[:, 0, j : j + 1], scale=scale[:, 0, j : j + 1],
+                    bias=shift[0][:, j : j + 1], scale=scale[:, 0, j : j + 1],
                 )
 
         def merge(c):
@@ -166,8 +166,8 @@ def tile_p2b_xcorr_pb_t_kernel(tc, h2, W3, g3, b3, m3, v3, Wc1, gc1, bc1, mc1, v
         wc1_codes, wc1_scales = weight_tiles("wc1")
         regroup(0)
         fold_scale()
-        fold_shift(0)
-        fold_shift(1)
+        fold_shift(nc.vector, 0)
+        fold_shift(nc.gpsimd, 1)
         w3_grouped = flip_weight(w3_rows, "w3_grouped")
         quantise(0)
         quantise_weight(w3_grouped, w3_codes, w3_scales, 0, 2)
@@ -217,6 +217,6 @@ def tile_p2b_xcorr_pb_t_kernel(tc, h2, W3, g3, b3, m3, v3, Wc1, gc1, bc1, mc1, v
         for j in range(PACK):
             nc.scalar.activation(
                 out=result[:, j, :], in_=xc_of[j // 2][:, j % 2, :], func=RELU,
-                bias=shift[:, 1, j : j + 1], scale=scale[:, 1, j : j + 1],
+                bias=shift[1][:, j : j + 1], scale=scale[:, 1, j : j + 1],
             )
             nc.sync.dma_start(out=out_rows[:, j, :], in_=result[:, j, :])

@@ -9,6 +9,7 @@ U32 = mybir.dt.uint32
 U8 = mybir.dt.uint8
 FP8X4 = mybir.dt.float8_e4m3fn_x4
 RELU = mybir.ActivationFunctionType.Relu
+SQRT = mybir.ActivationFunctionType.Sqrt
 
 P = 128
 PACK = 4
@@ -17,19 +18,18 @@ M_PTS = 32
 N_PTS = 128
 COLS = M_PTS * N_PTS
 BANK = 512
-CHUNKS = COLS // BANK
 WORDS = H // 2
 BN_EPS = 1e-5
-MERGE_LAG = 2
 
 FLOPS = 2 * H * H * (COLS + N_PTS)
 
 
 def tile_p2b_xcorr_pb_t_kernel(tc, h2, W3, g3, b3, m3, v3, Wc1, gc1, bc1, mc1, vc1, out):
     nc = tc.nc
+    PIECES = [(0, BANK // 2), (BANK // 2, BANK // 2)] + [(c, BANK) for c in range(BANK, COLS, BANK)]
+    N_PIECES = len(PIECES)
     with ExitStack() as ctx:
         keep = ctx.enter_context(tc.tile_pool(name="keep", bufs=1))
-        stage = ctx.enter_context(tc.tile_pool(name="stage", bufs=MERGE_LAG + 2))
         psum_w = ctx.enter_context(tc.psum_pool(name="psum_w", bufs=2))
         psum_x = ctx.enter_context(tc.psum_pool(name="psum_x", bufs=4))
         psum_y = ctx.enter_context(tc.psum_pool(name="psum_y", bufs=2))
@@ -37,155 +37,155 @@ def tile_p2b_xcorr_pb_t_kernel(tc, h2, W3, g3, b3, m3, v3, Wc1, gc1, bc1, mc1, v
 
         SLOT = 16
         bn_raw = keep.tile([P, 8, SLOT], BF16, name="bn_raw")
-
-        def load_vector(slot, vec):
-            nc.scalar.dma_start(out=bn_raw[:, slot, 0:PACK], in_=vec.rearrange("(p j) -> p j", j=PACK))
-
-        def load_late_vector(slot, vec):
-            nc.sync.dma_start(out=bn_raw[:, slot, 0:PACK], in_=vec.rearrange("(p j) -> p j", j=PACK))
-
         h2_rows = h2[0].rearrange("(p j) m n -> p j (m n)", j=PACK)
-        w3_rows = keep.tile([P, PACK * H], BF16, name="w3_rows")
-        wc1_rows = keep.tile([P, PACK * H], BF16, name="wc1_rows")
-        h2_raw = [keep.tile([P, PACK, BANK], BF16, name="h2_raw%d" % c) for c in range(CHUNKS)]
+        w3_rows = [keep.tile([P, 2 * H], BF16, name="w3_rows%d" % i) for i in range(2)]
+        wc1_rows = [keep.tile([P, 2 * H], BF16, name="wc1_rows%d" % i) for i in range(2)]
+        h2_raw = [keep.tile([P, PACK, width], BF16, name="h2_raw%d" % i) for i, (first, width) in enumerate(PIECES)]
 
-        def load_chunk(c):
-            nc.sync.dma_start(out=h2_raw[c][:], in_=h2_rows[:, :, c * BANK : (c + 1) * BANK])
+        def load_vector(queue, slot, vec):
+            queue.dma_start(out=bn_raw[:, slot, 0:PACK], in_=vec.rearrange("(p j) -> p j", j=PACK))
 
-        load_chunk(0)
-        nc.sync.dma_start(out=w3_rows[:], in_=W3.rearrange("(p j) h -> p (j h)", j=PACK))
-        load_chunk(1)
-        for slot, vec in ((0, v3), (1, vc1)):
-            load_vector(slot, vec)
+        def load_weight(rows, weight, i):
+            nc.sync.dma_start(
+                out=rows[i][:], in_=weight.rearrange("(p j) h -> p (j h)", j=PACK)[:, 2 * i * H : 2 * (i + 1) * H]
+            )
 
+        def load_piece(i):
+            first, width = PIECES[i]
+            nc.sync.dma_start(out=h2_raw[i][:], in_=h2_rows[:, :, first : first + width])
+
+        load_vector(nc.scalar, 0, v3)
+        load_vector(nc.scalar, 1, vc1)
+        for slot, vec in ((2, g3), (4, m3), (6, b3), (3, gc1)):
+            load_vector(nc.sync, slot, vec)
+        load_weight(w3_rows, W3, 0)
+        load_piece(0)
         warm = keep.tile([P, 1], F32, name="warm")
         nc.gpsimd.memset(warm[:], 1.0)
         nc.scalar.sqrt(out=warm[:], in_=warm[:])
-        for slot, vec in ((2, g3), (3, gc1), (4, m3), (6, b3)):
-            load_vector(slot, vec)
         ident = keep.tile([P, P], F32, name="ident")
         make_identity(nc, ident[:])
+        load_weight(w3_rows, W3, 1)
+        for i in range(1, N_PIECES):
+            load_piece(i)
+        load_weight(wc1_rows, Wc1, 0)
+        load_weight(wc1_rows, Wc1, 1)
+        load_vector(nc.sync, 5, mc1)
+        load_vector(nc.sync, 7, bc1)
 
-        for c in range(2, CHUNKS):
-            load_chunk(c)
-        nc.sync.dma_start(out=wc1_rows[:], in_=Wc1.rearrange("(p j) h -> p (j h)", j=PACK))
-        for slot, vec in ((5, mc1), (7, bc1)):
-            load_late_vector(slot, vec)
-
-        spread = keep.tile([P, 2, PACK], F32, name="spread")
         root = keep.tile([P, 2, PACK], F32, name="root")
         inverse = keep.tile([P, 2, PACK], F32, name="inverse")
         scale = keep.tile([P, 2, PACK], F32, name="scale")
+        gain_mean = keep.tile([P, PACK], F32, name="gain_mean")
         moved = [keep.tile([P, PACK], F32, name="moved%d" % i) for i in range(2)]
         shift = [keep.tile([P, PACK], F32, name="shift%d" % i) for i in range(2)]
-        nc.vector.tensor_scalar_add(out=spread[:], in0=bn_raw[:, 0:2, 0:PACK], scalar1=BN_EPS)
-        nc.scalar.sqrt(out=root[:], in_=spread[:])
+        nc.scalar.activation(out=root[:], in_=bn_raw[:, 0:2, 0:PACK], func=SQRT, bias=BN_EPS, scale=1.0)
 
-        def fold_scale():
-            nc.vector.reciprocal(out=inverse[:], in_=root[:])
-            nc.vector.tensor_mul(out=scale[:], in0=inverse[:], in1=bn_raw[:, 2:4, 0:PACK])
-
-        def fold_shift(engine, i):
-            engine.tensor_mul(out=moved[i][:], in0=scale[:, i, :], in1=bn_raw[:, 4 + i, 0:PACK])
-            engine.tensor_sub(out=shift[i][:], in0=bn_raw[:, 6 + i, 0:PACK], in1=moved[i][:])
-
-
-        def flip_weight(rows, name):
-            words = rows[:].bitcast(F32)
-            grouped = keep.tile([P, PACK * P * PACK], BF16, name=name, align_bytes=64)
-            grouped_words = grouped[:].bitcast(F32).rearrange("q (j p u) -> q j p u", j=PACK, u=2)
-            for j_pair in range(0, PACK, 2):
-                flipped = psum_w.tile([P, 2, 2, P], F32, name="flipped")
-                for j in range(2):
-                    first = (j_pair + j) * WORDS
-                    for u in range(2):
-                        nc.tensor.transpose(flipped[:, j, u, :], words[:, first + u : first + WORDS : 2], ident[:])
-                nc.scalar.copy(
-                    out=grouped_words[:, j_pair : j_pair + 2, :, :],
-                    in_=flipped[:].rearrange("q j u p -> q j p u"),
-                )
+        def flip_weight(rows, name, i):
+            words = rows[i][:].bitcast(F32)
+            grouped = keep.tile([P, 2 * P * PACK], BF16, name="%s%d" % (name, i), align_bytes=64)
+            flipped = psum_w.tile([P, 2, 2, P], F32, name="flipped")
+            for j in range(2):
+                for u in range(2):
+                    nc.tensor.transpose(flipped[:, j, u, :], words[:, j * WORDS + u : (j + 1) * WORDS : 2], ident[:])
+            nc.scalar.copy(
+                out=grouped[:].bitcast(F32).rearrange("q (j p u) -> q j p u", j=2, u=2),
+                in_=flipped[:].rearrange("q j u p -> q j p u"),
+            )
             return grouped
 
-        def weight_tiles(name):
-            codes = keep.tile([P, H], U32, name=name + "_codes", align_bytes=64)
-            scales = keep.tile([P, H], U8, name=name + "_scales", align_bytes=64)
+        def quantise_weight(grouped, name, i):
+            codes = keep.tile([P, 2 * P], U32, name="%s_codes%d" % (name, i), align_bytes=64)
+            scales = keep.tile([P, 2 * P], U8, name="%s_scales%d" % (name, i), align_bytes=64)
+            nc.vector.quantize_mx(out=codes[:].bitcast(FP8X4), scales=scales[:], in_=grouped[:])
             return codes, scales
 
-        def quantise_weight(grouped, codes, scales, first, count):
-            cols = slice(first * P, (first + count) * P)
-            nc.vector.quantize_mx(
-                out=codes[:, cols].bitcast(FP8X4), scales=scales[:, cols],
-                in_=grouped[:, first * P * PACK : (first + count) * P * PACK],
-            )
-
-        h2_codes = keep.tile([P, CHUNKS, BANK], U32, name="h2_codes", align_bytes=64)
-        h2_scales = keep.tile([P, CHUNKS, BANK], U8, name="h2_scales", align_bytes=64)
         h2_grouped = {}
+        h2_mx = {}
 
-        def regroup(c):
-            grouped = stage.tile([P, BANK, PACK], BF16, name="h2_grouped", align_bytes=64)
+        def regroup(i):
+            grouped = keep.tile([P, PIECES[i][1], PACK], BF16, name="h2_grouped%d" % i, align_bytes=64)
             nc.vector.tensor_copy(
                 out=grouped[:].rearrange("p (c i) j -> p c j i", i=4),
-                in_=h2_raw[c][:].rearrange("p j (c i) -> p c j i", i=4),
+                in_=h2_raw[i][:].rearrange("p j (c i) -> p c j i", i=4),
             )
-            h2_grouped[c] = grouped
+            h2_grouped[i] = grouped
 
-        def quantise(c):
+        def quantise(i):
+            codes = keep.tile([P, PIECES[i][1]], U32, name="h2_codes%d" % i, align_bytes=64)
+            scales = keep.tile([P, PIECES[i][1]], U8, name="h2_scales%d" % i, align_bytes=64)
             nc.vector.quantize_mx(
-                out=h2_codes[:, c, :].bitcast(FP8X4),
-                scales=h2_scales[:, c, :],
-                in_=h2_grouped[c][:].rearrange("p c j -> p (c j)"),
+                out=codes[:].bitcast(FP8X4), scales=scales[:], in_=h2_grouped[i][:].rearrange("p c j -> p (c j)")
             )
+            h2_mx[i] = (codes, scales)
 
         best = keep.tile([P, PACK, BANK], BF16, name="best")
-        h3_of = {0: best}
+        h3_of = {0: best[:, :, 0 : BANK // 2], 1: best[:, :, BANK // 2 : BANK]}
+        w3_mx = {}
 
-        def conv3(c):
-            if c > 0:
-                h3_of[c] = stage.tile([P, PACK, BANK], BF16, name="h3")
-            for j in range(PACK):
+        def conv3(i, js):
+            width = PIECES[i][1]
+            if i not in h3_of:
+                h3_tile = keep.tile([P, PACK, BANK], BF16, name="h3_%d" % i)
+                h3_of[i] = h3_tile[:]
+            codes, scales = h2_mx[i]
+            for j in js:
+                w_codes, w_scales = w3_mx[j // 2]
                 x3 = psum_x.tile([P, BANK], F32, name="x3")
                 nc.tensor.matmul_mx(
-                    out=x3[:],
-                    lhsT=w3_codes[:, j * P : (j + 1) * P].bitcast(FP8X4),
-                    lhsT_scale=w3_scales[:, j * P : (j + 1) * P],
-                    rhs=h2_codes[:, c, :].bitcast(FP8X4),
-                    rhs_scale=h2_scales[:, c, :],
+                    out=x3[:, 0:width],
+                    lhsT=w_codes[:, (j % 2) * P : (j % 2 + 1) * P].bitcast(FP8X4),
+                    lhsT_scale=w_scales[:, (j % 2) * P : (j % 2 + 1) * P],
+                    rhs=codes[:].bitcast(FP8X4),
+                    rhs_scale=scales[:],
                     start=True,
                     stop=True,
                 )
                 nc.scalar.activation(
-                    out=h3_of[c][:, j, :], in_=x3[:], func=RELU,
+                    out=h3_of[i][:, j, :], in_=x3[:, 0:width], func=RELU,
                     bias=shift[0][:, j : j + 1], scale=scale[:, 0, j : j + 1],
                 )
 
-        def merge(c):
-            nc.vector.tensor_max(out=best[:], in0=best[:], in1=h3_of[c][:])
+        def merge(i):
+            nc.vector.tensor_max(out=best[:], in0=best[:], in1=h3_of[i])
 
-        w3_codes, w3_scales = weight_tiles("w3")
-        wc1_codes, wc1_scales = weight_tiles("wc1")
+        w3_grouped = [flip_weight(w3_rows, "w3_grouped", i) for i in range(2)]
+        nc.vector.tensor_mul(out=gain_mean[:], in0=bn_raw[:, 2, 0:PACK], in1=bn_raw[:, 4, 0:PACK])
+        nc.vector.reciprocal(out=inverse[:], in_=root[:])
         regroup(0)
-        fold_scale()
-        fold_shift(nc.vector, 0)
-        fold_shift(nc.gpsimd, 1)
-        w3_grouped = flip_weight(w3_rows, "w3_grouped")
+        nc.vector.tensor_mul(out=scale[:], in0=inverse[:], in1=bn_raw[:, 2:4, 0:PACK])
+        nc.vector.tensor_mul(out=moved[0][:], in0=gain_mean[:], in1=inverse[:, 0, :])
         quantise(0)
-        quantise_weight(w3_grouped, w3_codes, w3_scales, 0, 2)
+        nc.vector.tensor_sub(out=shift[0][:], in0=bn_raw[:, 6, 0:PACK], in1=moved[0][:])
         regroup(1)
-        quantise_weight(w3_grouped, w3_codes, w3_scales, 2, 2)
+        w3_mx[0] = quantise_weight(w3_grouped[0], "w3", 0)
+        quantise(1)
+        conv3(0, (0, 1))
+        conv3(1, (0, 1))
         regroup(2)
-        for c in range(CHUNKS):
-            conv3(c)
-            if c == CHUNKS // 2 - 1:
-                wc1_grouped = flip_weight(wc1_rows, "wc1_grouped")
-            if c + 1 < CHUNKS:
-                quantise(c + 1)
-            if c + 1 - MERGE_LAG >= 1:
-                merge(c + 1 - MERGE_LAG)
-            if c + 3 < CHUNKS:
-                regroup(c + 3)
-        quantise_weight(wc1_grouped, wc1_codes, wc1_scales, 0, PACK)
-        merge(CHUNKS - 1)
+        w3_mx[1] = quantise_weight(w3_grouped[1], "w3", 1)
+        quantise(2)
+        conv3(0, (2, 3))
+        conv3(1, (2, 3))
+        regroup(3)
+        regroup(4)
+
+        for i in range(2, N_PIECES):
+            conv3(i, range(PACK))
+            if i == N_PIECES // 2:
+                wc1_grouped = [flip_weight(wc1_rows, "wc1_grouped", k) for k in range(2)]
+            if i + 1 < N_PIECES:
+                quantise(i + 1)
+            if i - 1 >= 2:
+                merge(i - 1)
+            if i + 3 < N_PIECES:
+                regroup(i + 3)
+            if i == N_PIECES - 3:
+                nc.vector.tensor_mul(out=moved[1][:], in0=scale[:, 1, :], in1=bn_raw[:, 5, 0:PACK])
+            if i == N_PIECES - 2:
+                nc.vector.tensor_sub(out=shift[1][:], in0=bn_raw[:, 7, 0:PACK], in1=moved[1][:])
+        wc1_mx = [quantise_weight(wc1_grouped[k], "wc1", k) for k in range(2)]
+        merge(N_PIECES - 1)
 
         two = keep.tile([P, PACK, 2 * N_PTS], BF16, name="two")
         nc.vector.tensor_max(out=two[:], in0=best[:, :, 0 : 2 * N_PTS], in1=best[:, :, 2 * N_PTS : BANK])
@@ -205,10 +205,11 @@ def tile_p2b_xcorr_pb_t_kernel(tc, h2, W3, g3, b3, m3, v3, Wc1, gc1, bc1, mc1, v
         result = keep.tile([P, PACK, N_PTS], F32, name="result")
         out_rows = out[0].rearrange("(p j) n -> p j n", j=PACK)
         for j in range(PACK):
+            w_codes, w_scales = wc1_mx[j // 2]
             nc.tensor.matmul_mx(
                 out=xc_of[j // 2][:, j % 2, :],
-                lhsT=wc1_codes[:, j * P : (j + 1) * P].bitcast(FP8X4),
-                lhsT_scale=wc1_scales[:, j * P : (j + 1) * P],
+                lhsT=w_codes[:, (j % 2) * P : (j % 2 + 1) * P].bitcast(FP8X4),
+                lhsT_scale=w_scales[:, (j % 2) * P : (j % 2 + 1) * P],
                 rhs=p_codes[:].bitcast(FP8X4),
                 rhs_scale=p_scales[:],
                 start=True,

@@ -28,6 +28,7 @@ def tile_p2b_xcorr_pb_t_kernel(tc, h2, W3, g3, b3, m3, v3, Wc1, gc1, bc1, mc1, v
     nc = tc.nc
     PIECES = [(0, BANK // 2), (BANK // 2, BANK // 2)] + [(c, BANK) for c in range(BANK, COLS, BANK)]
     N_PIECES = len(PIECES)
+    SCALAR_SHARE = {1: N_PTS, 2: N_PTS}
     with ExitStack() as ctx:
         keep = ctx.enter_context(tc.tile_pool(name="keep", bufs=1))
         psum_w = ctx.enter_context(tc.psum_pool(name="psum_w", bufs=2))
@@ -103,13 +104,18 @@ def tile_p2b_xcorr_pb_t_kernel(tc, h2, W3, g3, b3, m3, v3, Wc1, gc1, bc1, mc1, v
         h2_grouped = {}
         h2_mx = {}
 
-        def regroup(i):
-            grouped = keep.tile([P, PIECES[i][1], PACK], BF16, name="h2_grouped%d" % i, align_bytes=64)
-            nc.vector.tensor_copy(
-                out=grouped[:].rearrange("p (c i) j -> p c j i", i=4),
-                in_=h2_raw[i][:].rearrange("p j (c i) -> p c j i", i=4),
+        def regroup_part(copy, i, first, width):
+            copy(
+                out=h2_grouped[i][:, first : first + width, :].rearrange("p (c i) j -> p c j i", i=4),
+                in_=h2_raw[i][:, :, first : first + width].rearrange("p j (c i) -> p c j i", i=4),
             )
-            h2_grouped[i] = grouped
+
+        def regroup(i):
+            h2_grouped[i] = keep.tile([P, PIECES[i][1], PACK], BF16, name="h2_grouped%d" % i, align_bytes=64)
+            regroup_part(nc.vector.tensor_copy, i, 0, PIECES[i][1] - SCALAR_SHARE.get(i, 0))
+
+        def regroup_share(i):
+            regroup_part(nc.scalar.copy, i, PIECES[i][1] - SCALAR_SHARE[i], SCALAR_SHARE[i])
 
         def quantise(i):
             codes = keep.tile([P, PIECES[i][1]], U32, name="h2_codes%d" % i, align_bytes=64)
@@ -123,11 +129,14 @@ def tile_p2b_xcorr_pb_t_kernel(tc, h2, W3, g3, b3, m3, v3, Wc1, gc1, bc1, mc1, v
         h3_of = {0: best[:, :, 0 : BANK // 2], 1: best[:, :, BANK // 2 : BANK]}
         w3_mx = {}
 
-        def conv3(i, js):
-            width = PIECES[i][1]
-            if i not in h3_of:
-                h3_tile = keep.tile([P, PACK, BANK], BF16, name="h3_%d" % i)
-                h3_of[i] = h3_tile[:]
+        def conv3(i, js, first=0, width=None, h3=None):
+            if width is None:
+                width = PIECES[i][1]
+            if h3 is None:
+                if i not in h3_of:
+                    h3_tile = keep.tile([P, PACK, BANK], BF16, name="h3_%d" % i)
+                    h3_of[i] = h3_tile[:]
+                h3 = h3_of[i]
             codes, scales = h2_mx[i]
             for j in js:
                 w_codes, w_scales = w3_mx[j // 2]
@@ -136,20 +145,20 @@ def tile_p2b_xcorr_pb_t_kernel(tc, h2, W3, g3, b3, m3, v3, Wc1, gc1, bc1, mc1, v
                     out=x3[:, 0:width],
                     lhsT=w_codes[:, (j % 2) * P : (j % 2 + 1) * P].bitcast(FP8X4),
                     lhsT_scale=w_scales[:, (j % 2) * P : (j % 2 + 1) * P],
-                    rhs=codes[:].bitcast(FP8X4),
-                    rhs_scale=scales[:],
+                    rhs=codes[:, first : first + width].bitcast(FP8X4),
+                    rhs_scale=scales[:, first : first + width],
                     start=True,
                     stop=True,
                 )
                 nc.scalar.activation(
-                    out=h3_of[i][:, j, :], in_=x3[:, 0:width], func=RELU,
+                    out=h3[:, j, :], in_=x3[:, 0:width], func=RELU,
                     bias=shift[0][:, j : j + 1], scale=scale[:, 0, j : j + 1],
                 )
 
         def merge(i):
             nc.vector.tensor_max(out=best[:], in0=best[:], in1=h3_of[i])
 
-        w3_grouped = [flip_weight(w3_rows, "w3_grouped", i) for i in range(2)]
+        w3_grouped = [flip_weight(w3_rows, "w3_grouped", 0)]
         nc.vector.tensor_mul(out=gain_mean[:], in0=bn_raw[:, 2, 0:PACK], in1=bn_raw[:, 4, 0:PACK])
         nc.vector.reciprocal(out=inverse[:], in_=root[:])
         regroup(0)
@@ -158,11 +167,14 @@ def tile_p2b_xcorr_pb_t_kernel(tc, h2, W3, g3, b3, m3, v3, Wc1, gc1, bc1, mc1, v
         quantise(0)
         nc.vector.tensor_sub(out=shift[0][:], in0=bn_raw[:, 6, 0:PACK], in1=moved[0][:])
         regroup(1)
+        regroup_share(1)
+        w3_grouped.append(flip_weight(w3_rows, "w3_grouped", 1))
         w3_mx[0] = quantise_weight(w3_grouped[0], "w3", 0)
         quantise(1)
+        regroup(2)
+        regroup_share(2)
         conv3(0, (0, 1))
         conv3(1, (0, 1))
-        regroup(2)
         w3_mx[1] = quantise_weight(w3_grouped[1], "w3", 1)
         quantise(2)
         conv3(0, (2, 3))
@@ -170,8 +182,15 @@ def tile_p2b_xcorr_pb_t_kernel(tc, h2, W3, g3, b3, m3, v3, Wc1, gc1, bc1, mc1, v
         regroup(3)
         regroup(4)
 
+        h3_two = keep.tile([P, PACK, 2 * N_PTS], BF16, name="h3_two")
+        h3_one = [keep.tile([P, PACK, N_PTS], BF16, name="h3_one%d" % k) for k in range(2)]
         for i in range(2, N_PIECES):
-            conv3(i, range(PACK))
+            if i < N_PIECES - 1:
+                conv3(i, range(PACK))
+            else:
+                conv3(i, range(PACK), 0, 2 * N_PTS, h3_two[:])
+                conv3(i, range(PACK), 2 * N_PTS, N_PTS, h3_one[0][:])
+                conv3(i, range(PACK), 3 * N_PTS, N_PTS, h3_one[1][:])
             if i == N_PIECES // 2:
                 wc1_grouped = [flip_weight(wc1_rows, "wc1_grouped", k) for k in range(2)]
             if i + 1 < N_PIECES:
@@ -185,21 +204,33 @@ def tile_p2b_xcorr_pb_t_kernel(tc, h2, W3, g3, b3, m3, v3, Wc1, gc1, bc1, mc1, v
             if i == N_PIECES - 2:
                 nc.vector.tensor_sub(out=shift[1][:], in0=bn_raw[:, 7, 0:PACK], in1=moved[1][:])
         wc1_mx = [quantise_weight(wc1_grouped[k], "wc1", k) for k in range(2)]
-        merge(N_PIECES - 1)
 
         two = keep.tile([P, PACK, 2 * N_PTS], BF16, name="two")
-        nc.vector.tensor_max(out=two[:], in0=best[:, :, 0 : 2 * N_PTS], in1=best[:, :, 2 * N_PTS : BANK])
+        one = keep.tile([P, PACK, N_PTS], BF16, name="one")
         p_grouped = keep.tile([P, N_PTS, PACK], BF16, name="p_grouped", align_bytes=64)
-        nc.vector.tensor_max(
-            out=p_grouped[:],
-            in0=two[:, :, 0:N_PTS].rearrange("p j n -> p n j"),
-            in1=two[:, :, N_PTS : 2 * N_PTS].rearrange("p j n -> p n j"),
-        )
         p_codes = keep.tile([P, N_PTS], U32, name="p_codes", align_bytes=64)
         p_scales = keep.tile([P, N_PTS], U8, name="p_scales", align_bytes=64)
-        nc.vector.quantize_mx(
-            out=p_codes[:].bitcast(FP8X4), scales=p_scales[:], in_=p_grouped[:].rearrange("p n j -> p (n j)")
-        )
+        j_halves = (slice(0, PACK // 2), slice(PACK // 2, PACK))
+        n_halves = (slice(0, N_PTS // 2), slice(N_PTS // 2, N_PTS))
+        for js in j_halves:
+            nc.vector.tensor_max(out=two[:, js, :], in0=best[:, js, 0 : 2 * N_PTS], in1=best[:, js, 2 * N_PTS : BANK])
+        for js in j_halves:
+            nc.vector.tensor_max(out=two[:, js, :], in0=two[:, js, :], in1=h3_two[:, js, :])
+        for js in j_halves:
+            nc.vector.tensor_max(out=one[:, js, :], in0=two[:, js, 0:N_PTS], in1=two[:, js, N_PTS : 2 * N_PTS])
+        for js in j_halves:
+            nc.vector.tensor_max(out=one[:, js, :], in0=one[:, js, :], in1=h3_one[0][:, js, :])
+        for ns in n_halves:
+            nc.vector.tensor_max(
+                out=p_grouped[:, ns, :],
+                in0=one[:, :, ns].rearrange("p j n -> p n j"),
+                in1=h3_one[1][:, :, ns].rearrange("p j n -> p n j"),
+            )
+        for ns in n_halves:
+            nc.vector.quantize_mx(
+                out=p_codes[:, ns].bitcast(FP8X4), scales=p_scales[:, ns],
+                in_=p_grouped[:, ns, :].rearrange("p n j -> p (n j)"),
+            )
 
         xc_of = [psum_y.tile([P, PACK // 2, N_PTS], F32, name="xc") for half in range(2)]
         result = keep.tile([P, PACK, N_PTS], F32, name="result")

@@ -31,9 +31,8 @@ def tile_p2b_xcorr_pb_t_kernel(tc, h2, W3, g3, b3, m3, v3, Wc1, gc1, bc1, mc1, v
     SCALAR_SHARE = {1: N_PTS, 2: N_PTS}
     with ExitStack() as ctx:
         keep = ctx.enter_context(tc.tile_pool(name="keep", bufs=1))
-        psum_w = ctx.enter_context(tc.psum_pool(name="psum_w", bufs=2))
-        psum_x = ctx.enter_context(tc.psum_pool(name="psum_x", bufs=4))
-        psum_y = ctx.enter_context(tc.psum_pool(name="psum_y", bufs=2))
+        psum_x = ctx.enter_context(tc.psum_pool(name="psum_x", bufs=6))
+        psum_s = ctx.enter_context(tc.psum_pool(name="psum_s", bufs=2))
         ctx.enter_context(tc.manual_schedule())
 
         SLOT = 16
@@ -85,7 +84,7 @@ def tile_p2b_xcorr_pb_t_kernel(tc, h2, W3, g3, b3, m3, v3, Wc1, gc1, bc1, mc1, v
         def flip_weight(rows, name, i):
             words = rows[i][:].bitcast(F32)
             grouped = keep.tile([P, 2 * P * PACK], BF16, name="%s%d" % (name, i), align_bytes=64)
-            flipped = psum_w.tile([P, 2, 2, P], F32, name="flipped")
+            flipped = psum_s.tile([P, 2, 2, P], F32, name="side")
             for j in range(2):
                 for u in range(2):
                     nc.tensor.transpose(flipped[:, j, u, :], words[:, j * WORDS + u : (j + 1) * WORDS : 2], ident[:])
@@ -195,15 +194,17 @@ def tile_p2b_xcorr_pb_t_kernel(tc, h2, W3, g3, b3, m3, v3, Wc1, gc1, bc1, mc1, v
                 wc1_grouped = [flip_weight(wc1_rows, "wc1_grouped", k) for k in range(2)]
             if i + 1 < N_PIECES:
                 quantise(i + 1)
-            if i - 1 >= 2:
-                merge(i - 1)
+            if i - 2 >= 2:
+                merge(i - 2)
             if i + 3 < N_PIECES:
                 regroup(i + 3)
             if i == N_PIECES - 3:
                 nc.vector.tensor_mul(out=moved[1][:], in0=scale[:, 1, :], in1=bn_raw[:, 5, 0:PACK])
             if i == N_PIECES - 2:
                 nc.vector.tensor_sub(out=shift[1][:], in0=bn_raw[:, 7, 0:PACK], in1=moved[1][:])
-        wc1_mx = [quantise_weight(wc1_grouped[k], "wc1", k) for k in range(2)]
+        wc1_mx = [quantise_weight(wc1_grouped[0], "wc1", 0)]
+        merge(N_PIECES - 2)
+        wc1_mx.append(quantise_weight(wc1_grouped[1], "wc1", 1))
 
         two = keep.tile([P, PACK, 2 * N_PTS], BF16, name="two")
         one = keep.tile([P, PACK, N_PTS], BF16, name="one")
@@ -232,7 +233,7 @@ def tile_p2b_xcorr_pb_t_kernel(tc, h2, W3, g3, b3, m3, v3, Wc1, gc1, bc1, mc1, v
                 in_=p_grouped[:, ns, :].rearrange("p n j -> p (n j)"),
             )
 
-        xc_of = [psum_y.tile([P, PACK // 2, N_PTS], F32, name="xc") for half in range(2)]
+        xc_of = [psum_s.tile([P, PACK // 2, N_PTS], F32, name="side") for half in range(2)]
         result = keep.tile([P, PACK, N_PTS], F32, name="result")
         out_rows = out[0].rearrange("(p j) n -> p j n", j=PACK)
         for j in range(PACK):

@@ -20,6 +20,7 @@ COLS = M_PTS * N_PTS
 BANK = 512
 WORDS = H // 2
 BN_EPS = 1e-5
+RUN = 8
 
 FLOPS = 2 * H * H * (COLS + N_PTS)
 
@@ -105,8 +106,8 @@ def tile_p2b_xcorr_pb_t_kernel(tc, h2, W3, g3, b3, m3, v3, Wc1, gc1, bc1, mc1, v
 
         def regroup_part(copy, i, first, width):
             copy(
-                out=h2_grouped[i][:, first : first + width, :].rearrange("p (c i) j -> p c j i", i=4),
-                in_=h2_raw[i][:, :, first : first + width].rearrange("p j (c i) -> p c j i", i=4),
+                out=h2_grouped[i][:, first : first + width, :].rearrange("p (c i) j -> p c j i", i=RUN),
+                in_=h2_raw[i][:, :, first : first + width].rearrange("p j (c i) -> p c j i", i=RUN),
             )
 
         def regroup(i):

@@ -27,9 +27,11 @@ FLOPS = 2 * H * H * (COLS + N_PTS)
 
 def tile_p2b_xcorr_pb_t_kernel(tc, h2, W3, g3, b3, m3, v3, Wc1, gc1, bc1, mc1, vc1, out):
     nc = tc.nc
-    PIECES = [(0, BANK // 2), (BANK // 2, BANK // 2)] + [(c, BANK) for c in range(BANK, COLS, BANK)]
+    HALF = BANK // 2
+    N_HALVES = 4
+    PIECES = [(c * HALF, HALF) for c in range(N_HALVES)] + [(c, BANK) for c in range(N_HALVES * HALF, COLS, BANK)]
     N_PIECES = len(PIECES)
-    SCALAR_SHARE = {1: N_PTS, 2: N_PTS}
+    SCALAR_SHARE = {1: N_PTS, 7: N_PTS}
     with ExitStack() as ctx:
         keep = ctx.enter_context(tc.tile_pool(name="keep", bufs=1))
         psum_x = ctx.enter_context(tc.psum_pool(name="psum_x", bufs=6))
@@ -55,10 +57,8 @@ def tile_p2b_xcorr_pb_t_kernel(tc, h2, W3, g3, b3, m3, v3, Wc1, gc1, bc1, mc1, v
             first, width = PIECES[i]
             nc.sync.dma_start(out=h2_raw[i][:], in_=h2_rows[:, :, first : first + width])
 
-        load_vector(nc.scalar, 0, v3)
-        load_vector(nc.scalar, 1, vc1)
-        for slot, vec in ((2, g3), (4, m3), (6, b3), (3, gc1)):
-            load_vector(nc.sync, slot, vec)
+        for slot, vec in ((0, v3), (2, g3), (4, m3), (6, b3)):
+            load_vector(nc.scalar, slot, vec)
         load_weight(w3_rows, W3, 0)
         load_piece(0)
         warm = keep.tile([P, 1], F32, name="warm")
@@ -66,21 +66,33 @@ def tile_p2b_xcorr_pb_t_kernel(tc, h2, W3, g3, b3, m3, v3, Wc1, gc1, bc1, mc1, v
         nc.scalar.sqrt(out=warm[:], in_=warm[:])
         ident = keep.tile([P, P], F32, name="ident")
         make_identity(nc, ident[:])
+        load_piece(1)
         load_weight(w3_rows, W3, 1)
-        for i in range(1, N_PIECES):
+        for i in range(2, N_PIECES):
             load_piece(i)
         load_weight(wc1_rows, Wc1, 0)
         load_weight(wc1_rows, Wc1, 1)
-        load_vector(nc.sync, 5, mc1)
-        load_vector(nc.sync, 7, bc1)
+        for slot, vec in ((1, vc1), (3, gc1), (5, mc1), (7, bc1)):
+            load_vector(nc.sync, slot, vec)
 
-        root = keep.tile([P, 2, PACK], F32, name="root")
-        inverse = keep.tile([P, 2, PACK], F32, name="inverse")
-        scale = keep.tile([P, 2, PACK], F32, name="scale")
-        gain_mean = keep.tile([P, PACK], F32, name="gain_mean")
+        root = [keep.tile([P, PACK], F32, name="root%d" % i) for i in range(2)]
+        inverse = [keep.tile([P, PACK], F32, name="inverse%d" % i) for i in range(2)]
+        scale = [keep.tile([P, PACK], F32, name="scale%d" % i) for i in range(2)]
         moved = [keep.tile([P, PACK], F32, name="moved%d" % i) for i in range(2)]
         shift = [keep.tile([P, PACK], F32, name="shift%d" % i) for i in range(2)]
-        nc.scalar.activation(out=root[:], in_=bn_raw[:, 0:2, 0:PACK], func=SQRT, bias=BN_EPS, scale=1.0)
+
+        def take_root(i):
+            nc.scalar.activation(out=root[i][:], in_=bn_raw[:, i, 0:PACK], func=SQRT, bias=BN_EPS, scale=1.0)
+
+        def fold(i, step):
+            if step == 0:
+                nc.vector.reciprocal(out=inverse[i][:], in_=root[i][:])
+            elif step == 1:
+                nc.vector.tensor_mul(out=scale[i][:], in0=inverse[i][:], in1=bn_raw[:, 2 + i, 0:PACK])
+            elif step == 2:
+                nc.vector.tensor_mul(out=moved[i][:], in0=scale[i][:], in1=bn_raw[:, 4 + i, 0:PACK])
+            else:
+                nc.vector.tensor_sub(out=shift[i][:], in0=bn_raw[:, 6 + i, 0:PACK], in1=moved[i][:])
 
         def flip_weight(rows, name, i):
             words = rows[i][:].bitcast(F32)
@@ -110,8 +122,12 @@ def tile_p2b_xcorr_pb_t_kernel(tc, h2, W3, g3, b3, m3, v3, Wc1, gc1, bc1, mc1, v
                 in_=h2_raw[i][:, :, first : first + width].rearrange("p j (c i) -> p c j i", i=RUN),
             )
 
-        def regroup(i):
+        def start_regroup(i):
             h2_grouped[i] = keep.tile([P, PIECES[i][1], PACK], BF16, name="h2_grouped%d" % i, align_bytes=64)
+
+        def regroup(i):
+            if i not in h2_grouped:
+                start_regroup(i)
             regroup_part(nc.vector.tensor_copy, i, 0, PIECES[i][1] - SCALAR_SHARE.get(i, 0))
 
         def regroup_share(i):
@@ -126,7 +142,8 @@ def tile_p2b_xcorr_pb_t_kernel(tc, h2, W3, g3, b3, m3, v3, Wc1, gc1, bc1, mc1, v
             h2_mx[i] = (codes, scales)
 
         best = keep.tile([P, PACK, BANK], BF16, name="best")
-        h3_of = {0: best[:, :, 0 : BANK // 2], 1: best[:, :, BANK // 2 : BANK]}
+        h3_23 = keep.tile([P, PACK, BANK], BF16, name="h3_23")
+        h3_of = {0: best[:, :, 0:HALF], 1: best[:, :, HALF:BANK], 2: h3_23[:, :, 0:HALF], 3: h3_23[:, :, HALF:BANK]}
         w3_mx = {}
 
         def conv3(i, js, first=0, width=None, h3=None):
@@ -152,82 +169,103 @@ def tile_p2b_xcorr_pb_t_kernel(tc, h2, W3, g3, b3, m3, v3, Wc1, gc1, bc1, mc1, v
                 )
                 nc.scalar.activation(
                     out=h3[:, j, :], in_=x3[:, 0:width], func=RELU,
-                    bias=shift[0][:, j : j + 1], scale=scale[:, 0, j : j + 1],
+                    bias=shift[0][:, j : j + 1], scale=scale[0][:, j : j + 1],
                 )
 
-        def merge(i):
-            nc.vector.tensor_max(out=best[:], in0=best[:], in1=h3_of[i])
+        def merge(i, js=slice(0, PACK)):
+            h3 = h3_23 if i == N_HALVES - 1 else h3_of[i]
+            nc.vector.tensor_max(out=best[:, js, :], in0=best[:, js, :], in1=h3[:, js, :])
 
+        take_root(0)
+        fold(0, 0)
         w3_grouped = [flip_weight(w3_rows, "w3_grouped", 0)]
-        nc.vector.tensor_mul(out=gain_mean[:], in0=bn_raw[:, 2, 0:PACK], in1=bn_raw[:, 4, 0:PACK])
-        nc.vector.reciprocal(out=inverse[:], in_=root[:])
         regroup(0)
-        nc.vector.tensor_mul(out=scale[:], in0=inverse[:], in1=bn_raw[:, 2:4, 0:PACK])
-        nc.vector.tensor_mul(out=moved[0][:], in0=gain_mean[:], in1=inverse[:, 0, :])
-        quantise(0)
-        nc.vector.tensor_sub(out=shift[0][:], in0=bn_raw[:, 6, 0:PACK], in1=moved[0][:])
+        fold(0, 1)
+        if 1 in SCALAR_SHARE:
+            start_regroup(1)
+            regroup_share(1)
         regroup(1)
-        regroup_share(1)
+        fold(0, 2)
+        quantise(0)
+        fold(0, 3)
         w3_grouped.append(flip_weight(w3_rows, "w3_grouped", 1))
         w3_mx[0] = quantise_weight(w3_grouped[0], "w3", 0)
-        quantise(1)
-        regroup(2)
-        regroup_share(2)
         conv3(0, (0, 1))
+        quantise(1)
         conv3(1, (0, 1))
+        regroup(2)
         w3_mx[1] = quantise_weight(w3_grouped[1], "w3", 1)
-        quantise(2)
         conv3(0, (2, 3))
         conv3(1, (2, 3))
         regroup(3)
+        quantise(2)
+        if 4 in SCALAR_SHARE:
+            start_regroup(4)
+            regroup_share(4)
         regroup(4)
+        conv3(2, range(PACK))
+        quantise(3)
+        conv3(3, range(PACK))
+        quantise(4)
+        if 5 in SCALAR_SHARE:
+            start_regroup(5)
+            regroup_share(5)
+        regroup(5)
 
+        j_halves = (slice(0, PACK // 2), slice(PACK // 2, PACK))
         h3_two = keep.tile([P, PACK, 2 * N_PTS], BF16, name="h3_two")
         h3_one = [keep.tile([P, PACK, N_PTS], BF16, name="h3_one%d" % k) for k in range(2)]
-        for i in range(2, N_PIECES):
+        for i in range(N_HALVES, N_PIECES):
+            if i == N_HALVES + 1:
+                take_root(1)
+            if i + 2 in SCALAR_SHARE:
+                start_regroup(i + 2)
+                regroup_share(i + 2)
             if i < N_PIECES - 1:
                 conv3(i, range(PACK))
             else:
                 conv3(i, range(PACK), 0, 2 * N_PTS, h3_two[:])
                 conv3(i, range(PACK), 2 * N_PTS, N_PTS, h3_one[0][:])
                 conv3(i, range(PACK), 3 * N_PTS, N_PTS, h3_one[1][:])
-            if i == N_PIECES // 2:
+            if i == N_HALVES + 2:
                 wc1_grouped = [flip_weight(wc1_rows, "wc1_grouped", k) for k in range(2)]
+            if i + 2 < N_PIECES:
+                regroup(i + 2)
             if i + 1 < N_PIECES:
                 quantise(i + 1)
-            if i - 2 >= 2:
+            if i > N_HALVES + 1:
+                fold(1, i - N_HALVES - 2)
+            if i >= N_PIECES - 2:
+                for js in j_halves:
+                    merge(i - 2, js)
+            elif i - 2 >= N_HALVES - 1:
                 merge(i - 2)
-            if i + 3 < N_PIECES:
-                regroup(i + 3)
-            if i == N_PIECES - 3:
-                nc.vector.tensor_mul(out=moved[1][:], in0=scale[:, 1, :], in1=bn_raw[:, 5, 0:PACK])
-            if i == N_PIECES - 2:
-                nc.vector.tensor_sub(out=shift[1][:], in0=bn_raw[:, 7, 0:PACK], in1=moved[1][:])
-        wc1_mx = [quantise_weight(wc1_grouped[0], "wc1", 0)]
-        merge(N_PIECES - 2)
-        wc1_mx.append(quantise_weight(wc1_grouped[1], "wc1", 1))
+        wc1_mx = []
 
         two = keep.tile([P, PACK, 2 * N_PTS], BF16, name="two")
         one = keep.tile([P, PACK, N_PTS], BF16, name="one")
         p_grouped = keep.tile([P, N_PTS, PACK], BF16, name="p_grouped", align_bytes=64)
         p_codes = keep.tile([P, N_PTS], U32, name="p_codes", align_bytes=64)
         p_scales = keep.tile([P, N_PTS], U8, name="p_scales", align_bytes=64)
-        j_halves = (slice(0, PACK // 2), slice(PACK // 2, PACK))
         n_halves = (slice(0, N_PTS // 2), slice(N_PTS // 2, N_PTS))
+        for js in j_halves:
+            merge(N_PIECES - 2, js)
         for js in j_halves:
             nc.vector.tensor_max(out=two[:, js, :], in0=best[:, js, 0 : 2 * N_PTS], in1=best[:, js, 2 * N_PTS : BANK])
         for js in j_halves:
             nc.vector.tensor_max(out=two[:, js, :], in0=two[:, js, :], in1=h3_two[:, js, :])
         for js in j_halves:
+            if js is j_halves[1]:
+                nc.vector.tensor_max(out=h3_one[0][:], in0=h3_one[0][:], in1=h3_one[1][:])
             nc.vector.tensor_max(out=one[:, js, :], in0=two[:, js, 0:N_PTS], in1=two[:, js, N_PTS : 2 * N_PTS])
-        for js in j_halves:
-            nc.vector.tensor_max(out=one[:, js, :], in0=one[:, js, :], in1=h3_one[0][:, js, :])
+        wc1_mx.append(quantise_weight(wc1_grouped[0], "wc1", 0))
         for ns in n_halves:
             nc.vector.tensor_max(
                 out=p_grouped[:, ns, :],
                 in0=one[:, :, ns].rearrange("p j n -> p n j"),
-                in1=h3_one[1][:, :, ns].rearrange("p j n -> p n j"),
+                in1=h3_one[0][:, :, ns].rearrange("p j n -> p n j"),
             )
+        wc1_mx.append(quantise_weight(wc1_grouped[1], "wc1", 1))
         for ns in n_halves:
             nc.vector.quantize_mx(
                 out=p_codes[:, ns].bitcast(FP8X4), scales=p_scales[:, ns],
@@ -251,6 +289,6 @@ def tile_p2b_xcorr_pb_t_kernel(tc, h2, W3, g3, b3, m3, v3, Wc1, gc1, bc1, mc1, v
         for j in range(PACK):
             nc.scalar.activation(
                 out=result[:, j, :], in_=xc_of[j // 2][:, j % 2, :], func=RELU,
-                bias=shift[1][:, j : j + 1], scale=scale[:, 1, j : j + 1],
+                bias=shift[1][:, j : j + 1], scale=scale[1][:, j : j + 1],
             )
             nc.sync.dma_start(out=out_rows[:, j, :], in_=result[:, j, :])

@@ -31,7 +31,7 @@ def tile_p2b_xcorr_pb_t_kernel(tc, h2, W3, g3, b3, m3, v3, Wc1, gc1, bc1, mc1, v
     N_HALVES = 4
     PIECES = [(c * HALF, HALF) for c in range(N_HALVES)] + [(c, BANK) for c in range(N_HALVES * HALF, COLS, BANK)]
     N_PIECES = len(PIECES)
-    SCALAR_SHARE = {1: N_PTS, 7: N_PTS}
+    SCALAR_SHARE = {1: N_PTS, 6: N_PTS, 7: N_PTS}
     with ExitStack() as ctx:
         keep = ctx.enter_context(tc.tile_pool(name="keep", bufs=1))
         psum_x = ctx.enter_context(tc.psum_pool(name="psum_x", bufs=6))
@@ -57,10 +57,11 @@ def tile_p2b_xcorr_pb_t_kernel(tc, h2, W3, g3, b3, m3, v3, Wc1, gc1, bc1, mc1, v
             first, width = PIECES[i]
             nc.sync.dma_start(out=h2_raw[i][:], in_=h2_rows[:, :, first : first + width])
 
-        for slot, vec in ((0, v3), (2, g3), (4, m3), (6, b3)):
-            load_vector(nc.scalar, slot, vec)
+        load_vector(nc.scalar, 0, v3)
         load_weight(w3_rows, W3, 0)
         load_piece(0)
+        for slot, vec in ((2, g3), (4, m3), (6, b3)):
+            load_vector(nc.sync, slot, vec)
         warm = keep.tile([P, 1], F32, name="warm")
         nc.gpsimd.memset(warm[:], 1.0)
         nc.scalar.sqrt(out=warm[:], in_=warm[:])

@@ -31,7 +31,7 @@ def tile_p2b_xcorr_pb_t_kernel(tc, h2, W3, g3, b3, m3, v3, Wc1, gc1, bc1, mc1, v
     N_HALVES = 4
     PIECES = [(c * HALF, HALF) for c in range(N_HALVES)] + [(c, BANK) for c in range(N_HALVES * HALF, COLS, BANK)]
     N_PIECES = len(PIECES)
-    SCALAR_SHARE = {1: N_PTS, 6: N_PTS, 7: N_PTS}
+    SCALAR_SHARE = {1: N_PTS, 7: N_PTS}
     with ExitStack() as ctx:
         keep = ctx.enter_context(tc.tile_pool(name="keep", bufs=1))
         psum_x = ctx.enter_context(tc.psum_pool(name="psum_x", bufs=6))
@@ -71,10 +71,11 @@ def tile_p2b_xcorr_pb_t_kernel(tc, h2, W3, g3, b3, m3, v3, Wc1, gc1, bc1, mc1, v
         load_weight(w3_rows, W3, 1)
         for i in range(2, N_PIECES):
             load_piece(i)
+            if i == N_HALVES + 1:
+                for slot, vec in ((1, vc1), (3, gc1), (5, mc1), (7, bc1)):
+                    load_vector(nc.sync, slot, vec)
         load_weight(wc1_rows, Wc1, 0)
         load_weight(wc1_rows, Wc1, 1)
-        for slot, vec in ((1, vc1), (3, gc1), (5, mc1), (7, bc1)):
-            load_vector(nc.sync, slot, vec)
 
         root = [keep.tile([P, PACK], F32, name="root%d" % i) for i in range(2)]
         inverse = [keep.tile([P, PACK], F32, name="inverse%d" % i) for i in range(2)]
@@ -217,7 +218,7 @@ def tile_p2b_xcorr_pb_t_kernel(tc, h2, W3, g3, b3, m3, v3, Wc1, gc1, bc1, mc1, v
         h3_two = keep.tile([P, PACK, 2 * N_PTS], BF16, name="h3_two")
         h3_one = [keep.tile([P, PACK, N_PTS], BF16, name="h3_one%d" % k) for k in range(2)]
         for i in range(N_HALVES, N_PIECES):
-            if i == N_HALVES + 1:
+            if i == N_PIECES - 2:
                 take_root(1)
             if i + 2 in SCALAR_SHARE:
                 start_regroup(i + 2)
@@ -234,8 +235,8 @@ def tile_p2b_xcorr_pb_t_kernel(tc, h2, W3, g3, b3, m3, v3, Wc1, gc1, bc1, mc1, v
                 regroup(i + 2)
             if i + 1 < N_PIECES:
                 quantise(i + 1)
-            if i > N_HALVES + 1:
-                fold(1, i - N_HALVES - 2)
+            if i == N_PIECES - 1:
+                fold(1, 0)
             if i >= N_PIECES - 2:
                 for js in j_halves:
                     merge(i - 2, js)
@@ -253,13 +254,16 @@ def tile_p2b_xcorr_pb_t_kernel(tc, h2, W3, g3, b3, m3, v3, Wc1, gc1, bc1, mc1, v
             merge(N_PIECES - 2, js)
         for js in j_halves:
             nc.vector.tensor_max(out=two[:, js, :], in0=best[:, js, 0 : 2 * N_PTS], in1=best[:, js, 2 * N_PTS : BANK])
+        fold(1, 1)
         for js in j_halves:
             nc.vector.tensor_max(out=two[:, js, :], in0=two[:, js, :], in1=h3_two[:, js, :])
+        fold(1, 2)
         for js in j_halves:
             if js is j_halves[1]:
                 nc.vector.tensor_max(out=h3_one[0][:], in0=h3_one[0][:], in1=h3_one[1][:])
             nc.vector.tensor_max(out=one[:, js, :], in0=two[:, js, 0:N_PTS], in1=two[:, js, N_PTS : 2 * N_PTS])
         wc1_mx.append(quantise_weight(wc1_grouped[0], "wc1", 0))
+        fold(1, 3)
         for ns in n_halves:
             nc.vector.tensor_max(
                 out=p_grouped[:, ns, :],

@@ -9,7 +9,8 @@ U32 = mybir.dt.uint32
 U8 = mybir.dt.uint8
 FP8X4 = mybir.dt.float8_e4m3fn_x4
 RELU = mybir.ActivationFunctionType.Relu
-SQRT = mybir.ActivationFunctionType.Sqrt
+IDENTITY = mybir.ActivationFunctionType.Identity
+RSQRT = mybir.ActivationFunctionType.Abs_reciprocal_sqrt
 
 P = 128
 PACK = 4
@@ -64,7 +65,7 @@ def tile_p2b_xcorr_pb_t_kernel(tc, h2, W3, g3, b3, m3, v3, Wc1, gc1, bc1, mc1, v
             load_vector(nc.sync, slot, vec)
         warm = keep.tile([P, 1], F32, name="warm")
         nc.gpsimd.memset(warm[:], 1.0)
-        nc.scalar.sqrt(out=warm[:], in_=warm[:])
+        nc.scalar.activation(out=warm[:], in_=warm[:], func=RSQRT)
         ident = keep.tile([P, P], F32, name="ident")
         make_identity(nc, ident[:])
         load_piece(1)
@@ -77,24 +78,33 @@ def tile_p2b_xcorr_pb_t_kernel(tc, h2, W3, g3, b3, m3, v3, Wc1, gc1, bc1, mc1, v
         load_weight(wc1_rows, Wc1, 0)
         load_weight(wc1_rows, Wc1, 1)
 
-        root = [keep.tile([P, PACK], F32, name="root%d" % i) for i in range(2)]
         inverse = [keep.tile([P, PACK], F32, name="inverse%d" % i) for i in range(2)]
         scale = [keep.tile([P, PACK], F32, name="scale%d" % i) for i in range(2)]
-        moved = [keep.tile([P, PACK], F32, name="moved%d" % i) for i in range(2)]
         shift = [keep.tile([P, PACK], F32, name="shift%d" % i) for i in range(2)]
-
-        def take_root(i):
-            nc.scalar.activation(out=root[i][:], in_=bn_raw[:, i, 0:PACK], func=SQRT, bias=BN_EPS, scale=1.0)
+        moved = keep.tile([P, PACK], F32, name="moved")
+        minus_scale = keep.tile([P, PACK], F32, name="minus_scale")
+        nc.scalar.activation(out=inverse[0][:], in_=bn_raw[:, 0, 0:PACK], func=RSQRT, bias=BN_EPS, scale=1.0)
 
         def fold(i, step):
-            if step == 0:
-                nc.vector.reciprocal(out=inverse[i][:], in_=root[i][:])
-            elif step == 1:
-                nc.vector.tensor_mul(out=scale[i][:], in0=inverse[i][:], in1=bn_raw[:, 2 + i, 0:PACK])
+            if step == 1:
+                nc.vector.tensor_mul(out=scale[0][:], in0=inverse[0][:], in1=bn_raw[:, 2, 0:PACK])
             elif step == 2:
-                nc.vector.tensor_mul(out=moved[i][:], in0=scale[i][:], in1=bn_raw[:, 4 + i, 0:PACK])
+                nc.vector.tensor_mul(out=moved[:], in0=scale[0][:], in1=bn_raw[:, 4, 0:PACK])
             else:
-                nc.vector.tensor_sub(out=shift[i][:], in0=bn_raw[:, 6 + i, 0:PACK], in1=moved[i][:])
+                nc.vector.tensor_sub(out=shift[0][:], in0=bn_raw[:, 6, 0:PACK], in1=moved[:])
+
+        def fold_on_scalar():
+            nc.scalar.activation(out=inverse[1][:], in_=bn_raw[:, 1, 0:PACK], func=RSQRT, bias=BN_EPS, scale=1.0)
+            for j in range(PACK):
+                nc.scalar.activation(
+                    out=scale[1][:, j : j + 1], in_=bn_raw[:, 3, j : j + 1], func=IDENTITY, scale=inverse[1][:, j : j + 1]
+                )
+            nc.scalar.activation(out=minus_scale[:], in_=scale[1][:], func=IDENTITY, scale=-1.0)
+            for j in range(PACK):
+                nc.scalar.activation(
+                    out=shift[1][:, j : j + 1], in_=bn_raw[:, 5, j : j + 1], func=IDENTITY,
+                    bias=bn_raw[:, 7, j : j + 1], scale=minus_scale[:, j : j + 1],
+                )
 
         def flip_weight(rows, name, i):
             words = rows[i][:].bitcast(F32)
@@ -178,8 +188,6 @@ def tile_p2b_xcorr_pb_t_kernel(tc, h2, W3, g3, b3, m3, v3, Wc1, gc1, bc1, mc1, v
             h3 = h3_23 if i == N_HALVES - 1 else h3_of[i]
             nc.vector.tensor_max(out=best[:, js, :], in0=best[:, js, :], in1=h3[:, js, :])
 
-        take_root(0)
-        fold(0, 0)
         w3_grouped = [flip_weight(w3_rows, "w3_grouped", 0)]
         regroup(0)
         fold(0, 1)
@@ -218,8 +226,6 @@ def tile_p2b_xcorr_pb_t_kernel(tc, h2, W3, g3, b3, m3, v3, Wc1, gc1, bc1, mc1, v
         h3_two = keep.tile([P, PACK, 2 * N_PTS], BF16, name="h3_two")
         h3_one = [keep.tile([P, PACK, N_PTS], BF16, name="h3_one%d" % k) for k in range(2)]
         for i in range(N_HALVES, N_PIECES):
-            if i == N_PIECES - 2:
-                take_root(1)
             if i + 2 in SCALAR_SHARE:
                 start_regroup(i + 2)
                 regroup_share(i + 2)
@@ -235,13 +241,12 @@ def tile_p2b_xcorr_pb_t_kernel(tc, h2, W3, g3, b3, m3, v3, Wc1, gc1, bc1, mc1, v
                 regroup(i + 2)
             if i + 1 < N_PIECES:
                 quantise(i + 1)
-            if i == N_PIECES - 1:
-                fold(1, 0)
             if i >= N_PIECES - 2:
                 for js in j_halves:
                     merge(i - 2, js)
             elif i - 2 >= N_HALVES - 1:
                 merge(i - 2)
+        fold_on_scalar()
         wc1_mx = []
 
         two = keep.tile([P, PACK, 2 * N_PTS], BF16, name="two")
@@ -254,28 +259,20 @@ def tile_p2b_xcorr_pb_t_kernel(tc, h2, W3, g3, b3, m3, v3, Wc1, gc1, bc1, mc1, v
             merge(N_PIECES - 2, js)
         for js in j_halves:
             nc.vector.tensor_max(out=two[:, js, :], in0=best[:, js, 0 : 2 * N_PTS], in1=best[:, js, 2 * N_PTS : BANK])
-        fold(1, 1)
         for js in j_halves:
             nc.vector.tensor_max(out=two[:, js, :], in0=two[:, js, :], in1=h3_two[:, js, :])
-        fold(1, 2)
-        for js in j_halves:
-            if js is j_halves[1]:
-                nc.vector.tensor_max(out=h3_one[0][:], in0=h3_one[0][:], in1=h3_one[1][:])
-            nc.vector.tensor_max(out=one[:, js, :], in0=two[:, js, 0:N_PTS], in1=two[:, js, N_PTS : 2 * N_PTS])
+        nc.vector.tensor_max(out=h3_one[0][:], in0=h3_one[0][:], in1=h3_one[1][:])
+        nc.vector.tensor_max(out=one[:], in0=two[:, :, 0:N_PTS], in1=two[:, :, N_PTS : 2 * N_PTS])
         wc1_mx.append(quantise_weight(wc1_grouped[0], "wc1", 0))
-        fold(1, 3)
-        for ns in n_halves:
-            nc.vector.tensor_max(
-                out=p_grouped[:, ns, :],
-                in0=one[:, :, ns].rearrange("p j n -> p n j"),
-                in1=h3_one[0][:, :, ns].rearrange("p j n -> p n j"),
-            )
+        nc.vector.tensor_max(
+            out=p_grouped[:],
+            in0=one[:].rearrange("p j n -> p n j"),
+            in1=h3_one[0][:].rearrange("p j n -> p n j"),
+        )
         wc1_mx.append(quantise_weight(wc1_grouped[1], "wc1", 1))
-        for ns in n_halves:
-            nc.vector.quantize_mx(
-                out=p_codes[:, ns].bitcast(FP8X4), scales=p_scales[:, ns],
-                in_=p_grouped[:, ns, :].rearrange("p n j -> p (n j)"),
-            )
+        nc.vector.quantize_mx(
+            out=p_codes[:].bitcast(FP8X4), scales=p_scales[:], in_=p_grouped[:].rearrange("p n j -> p (n j)")
+        )
 
         xc_of = [psum_s.tile([P, PACK // 2, N_PTS], F32, name="side") for half in range(2)]
         result = keep.tile([P, PACK, N_PTS], F32, name="result")

@@ -255,14 +255,15 @@ def tile_p2b_xcorr_pb_t_kernel(tc, h2, W3, g3, b3, m3, v3, Wc1, gc1, bc1, mc1, v
         p_codes = keep.tile([P, N_PTS], U32, name="p_codes", align_bytes=64)
         p_scales = keep.tile([P, N_PTS], U8, name="p_scales", align_bytes=64)
         n_halves = (slice(0, N_PTS // 2), slice(N_PTS // 2, N_PTS))
-        for js in j_halves:
-            merge(N_PIECES - 2, js)
-        for js in j_halves:
-            nc.vector.tensor_max(out=two[:, js, :], in0=best[:, js, 0 : 2 * N_PTS], in1=best[:, js, 2 * N_PTS : BANK])
-        for js in j_halves:
-            nc.vector.tensor_max(out=two[:, js, :], in0=two[:, js, :], in1=h3_two[:, js, :])
-        nc.vector.tensor_max(out=h3_one[0][:], in0=h3_one[0][:], in1=h3_one[1][:])
+        t1 = keep.tile([P, PACK, N_PTS], BF16, name="t1")
+        merge(N_PIECES - 2, j_halves[0])
+        merge(N_PIECES - 2, j_halves[1])
+        nc.vector.tensor_max(out=t1[:], in0=h3_two[:, :, 0:N_PTS], in1=h3_two[:, :, N_PTS : 2 * N_PTS])
+        nc.vector.tensor_max(out=two[:, j_halves[0], :], in0=best[:, j_halves[0], 0 : 2 * N_PTS], in1=best[:, j_halves[0], 2 * N_PTS : BANK])
+        nc.vector.tensor_max(out=two[:, j_halves[1], :], in0=best[:, j_halves[1], 0 : 2 * N_PTS], in1=best[:, j_halves[1], 2 * N_PTS : BANK])
+        nc.vector.tensor_max(out=h3_one[0][:], in0=h3_one[0][:], in1=t1[:])
         nc.vector.tensor_max(out=one[:], in0=two[:, :, 0:N_PTS], in1=two[:, :, N_PTS : 2 * N_PTS])
+        nc.vector.tensor_max(out=h3_one[0][:], in0=h3_one[0][:], in1=h3_one[1][:])
         wc1_mx.append(quantise_weight(wc1_grouped[0], "wc1", 0))
         nc.vector.tensor_max(
             out=p_grouped[:],

@@ -32,7 +32,7 @@ def tile_p2b_xcorr_pb_t_kernel(tc, h2, W3, g3, b3, m3, v3, Wc1, gc1, bc1, mc1, v
     N_HALVES = 4
     PIECES = [(c * HALF, HALF) for c in range(N_HALVES)] + [(c, BANK) for c in range(N_HALVES * HALF, COLS, BANK)]
     N_PIECES = len(PIECES)
-    SCALAR_SHARE = {1: N_PTS, 7: N_PTS}
+    SCALAR_SHARE = {1: N_PTS}
     with ExitStack() as ctx:
         keep = ctx.enter_context(tc.tile_pool(name="keep", bufs=1))
         psum_x = ctx.enter_context(tc.psum_pool(name="psum_x", bufs=6))

from contextlib import ExitStack

import concourse.mybir as mybir
from concourse.masks import make_identity

BF16 = mybir.dt.bfloat16
F32 = mybir.dt.float32
U32 = mybir.dt.uint32
U8 = mybir.dt.uint8
FP8X4 = mybir.dt.float8_e4m3fn_x4
RELU = mybir.ActivationFunctionType.Relu
IDENTITY = mybir.ActivationFunctionType.Identity
RSQRT = mybir.ActivationFunctionType.Abs_reciprocal_sqrt

P = 128
PACK = 4
H = P * PACK
M_PTS = 32
N_PTS = 128
COLS = M_PTS * N_PTS
BANK = 512
WORDS = H // 2
BN_EPS = 1e-5
RUN = 8

FLOPS = 2 * H * H * (COLS + N_PTS)


def tile_p2b_xcorr_pb_t_kernel(tc, h2, W3, g3, b3, m3, v3, Wc1, gc1, bc1, mc1, vc1, out):
    nc = tc.nc
    HALF = BANK // 2
    N_HALVES = 4
    PIECES = [(c * HALF, HALF) for c in range(N_HALVES)] + [(c, BANK) for c in range(N_HALVES * HALF, COLS, BANK)]
    N_PIECES = len(PIECES)
    SCALAR_SHARE = {1: N_PTS}
    with ExitStack() as ctx:
        keep = ctx.enter_context(tc.tile_pool(name="keep", bufs=1))
        psum_x = ctx.enter_context(tc.psum_pool(name="psum_x", bufs=6))
        psum_s = ctx.enter_context(tc.psum_pool(name="psum_s", bufs=2))
        ctx.enter_context(tc.manual_schedule())

        SLOT = 16
        bn_raw = keep.tile([P, 8, SLOT], BF16, name="bn_raw")
        h2_rows = h2[0].rearrange("(p j) m n -> p j (m n)", j=PACK)
        w3_rows = [keep.tile([P, 2 * H], BF16, name="w3_rows%d" % i) for i in range(2)]
        wc1_rows = [keep.tile([P, 2 * H], BF16, name="wc1_rows%d" % i) for i in range(2)]
        h2_raw = [keep.tile([P, PACK, width], BF16, name="h2_raw%d" % i) for i, (first, width) in enumerate(PIECES)]

        def load_vector(queue, slot, vec):
            queue.dma_start(out=bn_raw[:, slot, 0:PACK], in_=vec.rearrange("(p j) -> p j", j=PACK))

        def load_weight(rows, weight, i):
            nc.sync.dma_start(
                out=rows[i][:], in_=weight.rearrange("(p j) h -> p (j h)", j=PACK)[:, 2 * i * H : 2 * (i + 1) * H]
            )

        def load_piece(i):
            first, width = PIECES[i]
            nc.sync.dma_start(out=h2_raw[i][:], in_=h2_rows[:, :, first : first + width])

        load_vector(nc.scalar, 0, v3)
        load_weight(w3_rows, W3, 0)
        load_piece(0)
        for slot, vec in ((2, g3), (4, m3), (6, b3)):
            load_vector(nc.sync, slot, vec)
        warm = keep.tile([P, 1], F32, name="warm")
        nc.gpsimd.memset(warm[:], 1.0)
        nc.scalar.activation(out=warm[:], in_=warm[:], func=RSQRT)
        ident = keep.tile([P, P], F32, name="ident")
        make_identity(nc, ident[:])
        load_piece(1)
        load_weight(w3_rows, W3, 1)
        for i in range(2, N_PIECES):
            load_piece(i)
            if i == N_HALVES + 1:
                for slot, vec in ((1, vc1), (3, gc1), (5, mc1), (7, bc1)):
                    load_vector(nc.sync, slot, vec)
        load_weight(wc1_rows, Wc1, 0)
        load_weight(wc1_rows, Wc1, 1)

        inverse = [keep.tile([P, PACK], F32, name="inverse%d" % i) for i in range(2)]
        scale = [keep.tile([P, PACK], F32, name="scale%d" % i) for i in range(2)]
        shift = [keep.tile([P, PACK], F32, name="shift%d" % i) for i in range(2)]
        moved = keep.tile([P, PACK], F32, name="moved")
        minus_scale = keep.tile([P, PACK], F32, name="minus_scale")
        nc.scalar.activation(out=inverse[0][:], in_=bn_raw[:, 0, 0:PACK], func=RSQRT, bias=BN_EPS, scale=1.0)

        def fold(i, step):
            if step == 1:
                nc.vector.tensor_mul(out=scale[0][:], in0=inverse[0][:], in1=bn_raw[:, 2, 0:PACK])
            elif step == 2:
                nc.vector.tensor_mul(out=moved[:], in0=scale[0][:], in1=bn_raw[:, 4, 0:PACK])
            else:
                nc.vector.tensor_sub(out=shift[0][:], in0=bn_raw[:, 6, 0:PACK], in1=moved[:])

        def fold_on_scalar():
            nc.scalar.activation(out=inverse[1][:], in_=bn_raw[:, 1, 0:PACK], func=RSQRT, bias=BN_EPS, scale=1.0)
            for j in range(PACK):
                nc.scalar.activation(
                    out=scale[1][:, j : j + 1], in_=bn_raw[:, 3, j : j + 1], func=IDENTITY, scale=inverse[1][:, j : j + 1]
                )
            nc.scalar.activation(out=minus_scale[:], in_=scale[1][:], func=IDENTITY, scale=-1.0)
            for j in range(PACK):
                nc.scalar.activation(
                    out=shift[1][:, j : j + 1], in_=bn_raw[:, 5, j : j + 1], func=IDENTITY,
                    bias=bn_raw[:, 7, j : j + 1], scale=minus_scale[:, j : j + 1],
                )

        def flip_weight(rows, name, i):
            words = rows[i][:].bitcast(F32)
            grouped = keep.tile([P, 2 * P * PACK], BF16, name="%s%d" % (name, i), align_bytes=64)
            flipped = psum_s.tile([P, 2, 2, P], F32, name="side")
            for j in range(2):
                for u in range(2):
                    nc.tensor.transpose(flipped[:, j, u, :], words[:, j * WORDS + u : (j + 1) * WORDS : 2], ident[:])
            nc.scalar.copy(
                out=grouped[:].bitcast(F32).rearrange("q (j p u) -> q j p u", j=2, u=2),
                in_=flipped[:].rearrange("q j u p -> q j p u"),
            )
            return grouped

        def quantise_weight(grouped, name, i):
            codes = keep.tile([P, 2 * P], U32, name="%s_codes%d" % (name, i), align_bytes=64)
            scales = keep.tile([P, 2 * P], U8, name="%s_scales%d" % (name, i), align_bytes=64)
            nc.vector.quantize_mx(out=codes[:].bitcast(FP8X4), scales=scales[:], in_=grouped[:])
            return codes, scales

        h2_grouped = {}
        h2_mx = {}

        def regroup_part(copy, i, first, width):
            copy(
                out=h2_grouped[i][:, first : first + width, :].rearrange("p (c i) j -> p c j i", i=RUN),
                in_=h2_raw[i][:, :, first : first + width].rearrange("p j (c i) -> p c j i", i=RUN),
            )

        def start_regroup(i):
            h2_grouped[i] = keep.tile([P, PIECES[i][1], PACK], BF16, name="h2_grouped%d" % i, align_bytes=64)

        def regroup(i):
            if i not in h2_grouped:
                start_regroup(i)
            regroup_part(nc.vector.tensor_copy, i, 0, PIECES[i][1] - SCALAR_SHARE.get(i, 0))

        def regroup_share(i):
            regroup_part(nc.scalar.copy, i, PIECES[i][1] - SCALAR_SHARE[i], SCALAR_SHARE[i])

        def quantise(i):
            codes = keep.tile([P, PIECES[i][1]], U32, name="h2_codes%d" % i, align_bytes=64)
            scales = keep.tile([P, PIECES[i][1]], U8, name="h2_scales%d" % i, align_bytes=64)
            nc.vector.quantize_mx(
                out=codes[:].bitcast(FP8X4), scales=scales[:], in_=h2_grouped[i][:].rearrange("p c j -> p (c j)")
            )
            h2_mx[i] = (codes, scales)

        best = keep.tile([P, PACK, BANK], BF16, name="best")
        h3_23 = keep.tile([P, PACK, BANK], BF16, name="h3_23")
        h3_of = {0: best[:, :, 0:HALF], 1: best[:, :, HALF:BANK], 2: h3_23[:, :, 0:HALF], 3: h3_23[:, :, HALF:BANK]}
        w3_mx = {}

        def conv3(i, js, first=0, width=None, h3=None):
            if width is None:
                width = PIECES[i][1]
            if h3 is None:
                if i not in h3_of:
                    h3_tile = keep.tile([P, PACK, BANK], BF16, name="h3_%d" % i)
                    h3_of[i] = h3_tile[:]
                h3 = h3_of[i]
            codes, scales = h2_mx[i]
            for j in js:
                w_codes, w_scales = w3_mx[j // 2]
                x3 = psum_x.tile([P, BANK], F32, name="x3")
                nc.tensor.matmul_mx(
                    out=x3[:, 0:width],
                    lhsT=w_codes[:, (j % 2) * P : (j % 2 + 1) * P].bitcast(FP8X4),
                    lhsT_scale=w_scales[:, (j % 2) * P : (j % 2 + 1) * P],
                    rhs=codes[:, first : first + width].bitcast(FP8X4),
                    rhs_scale=scales[:, first : first + width],
                    start=True,
                    stop=True,
                )
                nc.scalar.activation(
                    out=h3[:, j, :], in_=x3[:, 0:width], func=RELU,
                    bias=shift[0][:, j : j + 1], scale=scale[0][:, j : j + 1],
                )

        def merge(i, js=slice(0, PACK)):
            h3 = h3_23 if i == N_HALVES - 1 else h3_of[i]
            nc.vector.tensor_max(out=best[:, js, :], in0=best[:, js, :], in1=h3[:, js, :])

        w3_grouped = [flip_weight(w3_rows, "w3_grouped", 0)]
        regroup(0)
        fold(0, 1)
        if 1 in SCALAR_SHARE:
            start_regroup(1)
            regroup_share(1)
        regroup(1)
        fold(0, 2)
        quantise(0)
        fold(0, 3)
        w3_grouped.append(flip_weight(w3_rows, "w3_grouped", 1))
        w3_mx[0] = quantise_weight(w3_grouped[0], "w3", 0)
        conv3(0, (0, 1))
        quantise(1)
        conv3(1, (0, 1))
        regroup(2)
        w3_mx[1] = quantise_weight(w3_grouped[1], "w3", 1)
        conv3(0, (2, 3))
        conv3(1, (2, 3))
        regroup(3)
        quantise(2)
        if 4 in SCALAR_SHARE:
            start_regroup(4)
            regroup_share(4)
        regroup(4)
        conv3(2, range(PACK))
        quantise(3)
        conv3(3, range(PACK))
        quantise(4)
        if 5 in SCALAR_SHARE:
            start_regroup(5)
            regroup_share(5)
        regroup(5)

        j_halves = (slice(0, PACK // 2), slice(PACK // 2, PACK))
        h3_two = keep.tile([P, PACK, 2 * N_PTS], BF16, name="h3_two")
        h3_one = [keep.tile([P, PACK, N_PTS], BF16, name="h3_one%d" % k) for k in range(2)]
        for i in range(N_HALVES, N_PIECES):
            if i + 2 in SCALAR_SHARE:
                start_regroup(i + 2)
                regroup_share(i + 2)
            if i < N_PIECES - 1:
                conv3(i, range(PACK))
            else:
                conv3(i, range(PACK), 0, 2 * N_PTS, h3_two[:])
                conv3(i, range(PACK), 2 * N_PTS, N_PTS, h3_one[0][:])
                conv3(i, range(PACK), 3 * N_PTS, N_PTS, h3_one[1][:])
            if i == N_HALVES + 2:
                wc1_grouped = [flip_weight(wc1_rows, "wc1_grouped", k) for k in range(2)]
            if i + 2 < N_PIECES:
                regroup(i + 2)
            if i + 1 < N_PIECES:
                quantise(i + 1)
            if i >= N_PIECES - 2:
                for js in j_halves:
                    merge(i - 2, js)
            elif i - 2 >= N_HALVES - 1:
                merge(i - 2)
        fold_on_scalar()
        wc1_mx = []

        two = keep.tile([P, PACK, 2 * N_PTS], BF16, name="two")
        one = keep.tile([P, PACK, N_PTS], BF16, name="one")
        p_grouped = keep.tile([P, N_PTS, PACK], BF16, name="p_grouped", align_bytes=64)
        p_codes = keep.tile([P, N_PTS], U32, name="p_codes", align_bytes=64)
        p_scales = keep.tile([P, N_PTS], U8, name="p_scales", align_bytes=64)
        n_halves = (slice(0, N_PTS // 2), slice(N_PTS // 2, N_PTS))
        t1 = keep.tile([P, PACK, N_PTS], BF16, name="t1")
        merge(N_PIECES - 2, j_halves[0])
        merge(N_PIECES - 2, j_halves[1])
        nc.vector.tensor_max(out=t1[:], in0=h3_two[:, :, 0:N_PTS], in1=h3_two[:, :, N_PTS : 2 * N_PTS])
        nc.vector.tensor_max(out=two[:, j_halves[0], :], in0=best[:, j_halves[0], 0 : 2 * N_PTS], in1=best[:, j_halves[0], 2 * N_PTS : BANK])
        nc.vector.tensor_max(out=two[:, j_halves[1], :], in0=best[:, j_halves[1], 0 : 2 * N_PTS], in1=best[:, j_halves[1], 2 * N_PTS : BANK])
        nc.vector.tensor_max(out=h3_one[0][:], in0=h3_one[0][:], in1=t1[:])
        nc.vector.tensor_max(out=one[:], in0=two[:, :, 0:N_PTS], in1=two[:, :, N_PTS : 2 * N_PTS])
        nc.vector.tensor_max(out=h3_one[0][:], in0=h3_one[0][:], in1=h3_one[1][:])
        wc1_mx.append(quantise_weight(wc1_grouped[0], "wc1", 0))
        nc.vector.tensor_max(
            out=p_grouped[:],
            in0=one[:].rearrange("p j n -> p n j"),
            in1=h3_one[0][:].rearrange("p j n -> p n j"),
        )
        wc1_mx.append(quantise_weight(wc1_grouped[1], "wc1", 1))
        nc.vector.quantize_mx(
            out=p_codes[:].bitcast(FP8X4), scales=p_scales[:], in_=p_grouped[:].rearrange("p n j -> p (n j)")
        )

        xc_of = [psum_s.tile([P, PACK // 2, N_PTS], F32, name="side") for half in range(2)]
        result = keep.tile([P, PACK, N_PTS], F32, name="result")
        out_rows = out[0].rearrange("(p j) n -> p j n", j=PACK)
        for j in range(PACK):
            w_codes, w_scales = wc1_mx[j // 2]
            nc.tensor.matmul_mx(
                out=xc_of[j // 2][:, j % 2, :],
                lhsT=w_codes[:, (j % 2) * P : (j % 2 + 1) * P].bitcast(FP8X4),
                lhsT_scale=w_scales[:, (j % 2) * P : (j % 2 + 1) * P],
                rhs=p_codes[:].bitcast(FP8X4),
                rhs_scale=p_scales[:],
                start=True,
                stop=True,
            )
        for j in range(PACK):
            nc.scalar.activation(
                out=result[:, j, :], in_=xc_of[j // 2][:, j % 2, :], func=RELU,
                bias=shift[1][:, j : j + 1], scale=scale[1][:, j : j + 1],
            )
            nc.sync.dma_start(out=out_rows[:, j, :], in_=result[:, j, :])
